import numpy as np
import ml_dtypes


def mxq(x, axis, fmt="e4m3"):
    dtype, down = {"e4m3": (ml_dtypes.float8_e4m3fn, 7), "e5m2": (ml_dtypes.float8_e5m2, 14)}[fmt]
    v = np.moveaxis(np.asarray(x, np.float32).astype(ml_dtypes.bfloat16).astype(np.float64), axis, -1)
    blocks = v.reshape(v.shape[:-1] + (-1, 32))
    amax = np.abs(blocks).max(-1, keepdims=True)
    byte = np.maximum(np.where(amax > 0, np.frexp(amax)[1] - 1 + 127, 0) - down, 1)
    scale = np.exp2(byte - 127.0)
    codes = (blocks / scale).astype(np.float32).astype(dtype).astype(np.float64)
    return np.moveaxis((codes * scale).reshape(v.shape), -1, axis)


WIDE = False


def mx_kscale(k):
    if not WIDE:
        return np.ones(k)
    levels = np.array([10, -10, 5, -5, 0])
    if k % 512:
        return np.exp2(np.random.permutation(np.resize(levels, k // 32))).repeat(32)
    a = np.empty((k // 512, 16))
    for p in range(k // 512):
        a[p, :8] = np.random.permutation(np.resize(levels, 8))
        for g in range(8):
            far = levels[np.abs(levels - a[p, g]) >= 10]
            a[p, g + 8] = far[np.random.randint(len(far))]
    return np.exp2(a.ravel()).repeat(32)


BF16 = ml_dtypes.bfloat16


def bf(x):
    return np.asarray(x, np.float32).astype(BF16)


def f64(x):
    return np.asarray(x).astype(np.float64)


B, IN, OUT = 512, 2048, 2048


def setup_inputs():
    s = mx_kscale(IN)
    return {"input_data": bf(np.random.standard_normal((B, IN)) * s),
            "weight": bf(np.random.standard_normal((OUT, IN)) / np.sqrt(IN) / s),
            "bias": bf(np.random.standard_normal(OUT) * 0.5),
            "prev_grad": bf(np.random.standard_normal((OUT, IN)) / np.sqrt(IN) / s),
            "prev_bias_grad": bf(np.random.standard_normal(OUT) * 0.5),
            "lr_samples": bf(np.random.uniform(0.1, 1.0, B))}


def core(input_data, weight, bias, prev_grad, prev_bias_grad, lr_samples):
    xq = mxq(f64(input_data), 1, "e4m3")
    base = (xq @ mxq(f64(weight), 1, "e4m3").T) + f64(bias)
    pert = (xq @ mxq(f64(prev_grad), 1, "e4m3").T) + f64(prev_bias_grad)
    return base - f64(lr_samples)[:, None] * pert


def e4m3fn_bytes(y):
    return np.clip(np.asarray(y, np.float64), -448.0, 448.0).astype(np.float32).astype(ml_dtypes.float8_e4m3fn).view(np.uint8)


Y_SCALE = 170.0


def reference(input_data, weight, bias, prev_grad, prev_bias_grad, lr_samples):
    out = core(input_data, weight, bias, prev_grad, prev_bias_grad, lr_samples)
    return out, e4m3fn_bytes(out * Y_SCALE)

@@ -1,0 +1,295 @@
+from contextlib import ExitStack
+
+import concourse.mybir as mybir
+from concourse.masks import make_identity
+
+B, IN, OUT = 512, 2048, 2048
+FLOPS = 2 * 2 * B * IN * OUT
+Y_SCALE = 170.0
+
+F32 = mybir.dt.float32
+BF16 = mybir.dt.bfloat16
+U32 = mybir.dt.uint32
+U8 = mybir.dt.uint8
+FP8X4 = mybir.dt.float8_e4m3fn_x4
+FP8 = mybir.dt.float8_e4m3fn
+ALU = mybir.AluOpType
+ACT = mybir.ActivationFunctionType
+
+P = 128
+PASSES = IN // 512
+NB = B // P
+
+CHUNKS = (256, 256, 512, 512, 512)
+DEI_DEFAULT = "n"
+DEI = {}
+CO_DEFAULT = "ssss"
+CO = {}
+DEV = "sv"
+RAW_BUFS = 12
+DEI_BUFS = 8
+LOAD_AHEAD = 12
+DEI_AHEAD = 2
+D_FIRST = 8
+D_PER_T = 2
+CAST_ON = "s"
+LEADS = (5, 7, 9, 11)
+LEAD_STEADY = 8
+
+
+def tile_optimizedlinear_kernel(tc, input_data, weight, bias, prev_grad, prev_bias_grad, lr_samples, out_0, out_1):
+    nc = tc.nc
+    starts = [sum(CHUNKS[:c]) for c in range(len(CHUNKS))]
+
+    units = [(input_data, 0, B)]
+    for c, wdt in enumerate(CHUNKS):
+        units.append((weight, starts[c], wdt))
+        units.append((prev_grad, starts[c], wdt))
+    tiles = [(u, rt) for u in range(len(units)) for rt in range(units[u][2] // P)]
+    truns = [(u, part) for u in range(len(units)) for part in range(units[u][2] // 256)]
+    NT = len(truns)
+    mruns = []
+    for c, wdt in enumerate(CHUNKS):
+        per = 512 // wdt
+        for i0 in range(0, NB, per):
+            mruns.append([(c, i) for i in range(i0, i0 + per)])
+    NM = len(mruns)
+    ditems = [(c, i) for c in range(len(CHUNKS)) for i in range(NB)]
+
+    seq = [("D", c, i) for (c, i) in ditems[:D_FIRST]]
+    dleft = ditems[D_FIRST:]
+    done_t = 0
+    for j in range(NM):
+        want = LEADS[j] if j < len(LEADS) else min(NT, LEAD_STEADY + j)
+        while done_t < want:
+            seq.append(("T", done_t))
+            done_t += 1
+            for (c, i) in dleft[:D_PER_T]:
+                seq.append(("D", c, i))
+            dleft = dleft[D_PER_T:]
+        seq.append(("M", j))
+
+    with ExitStack() as ctx:
+        const = ctx.enter_context(tc.tile_pool(name="const", bufs=1))
+        rawp = ctx.enter_context(tc.tile_pool(name="rawp", bufs=RAW_BUFS))
+        deip = ctx.enter_context(tc.tile_pool(name="deip", bufs=DEI_BUFS))
+        grpp = ctx.enter_context(tc.tile_pool(name="grpp", bufs=3))
+        codp = ctx.enter_context(tc.tile_pool(name="codp", bufs=3))
+        epp = ctx.enter_context(tc.tile_pool(name="epp", bufs=3))
+        tpp = ctx.enter_context(tc.psum_pool(name="tpp", bufs=4))
+        accp = ctx.enter_context(tc.psum_pool(name="accp", bufs=4))
+        ctx.enter_context(tc.manual_schedule())
+
+        raw = {}
+        dei = {}
+        grp = {}
+        cod = {}
+        acc = {}
+        tmp = {}
+        state = {"loaded": 0, "used": 0, "nd": 0}
+
+        freed = set()
+
+        def load():
+            n = state["loaded"]
+            if n >= len(tiles) or n - state["used"] >= LOAD_AHEAD:
+                return
+            if n >= RAW_BUFS and tiles[n - RAW_BUFS] not in freed:
+                return
+            u, rt = tiles[n]
+            state["loaded"] += 1
+            src, r0, rows = units[u]
+            tl = rawp.tile([P, IN], BF16, name="raw")
+            raw[(u, rt)] = tl
+            nc.sync.dma_start(out=tl[:], in_=src[r0 + rt * P:r0 + (rt + 1) * P, :])
+
+        lmat = const.tile([P, B], BF16, name="lmat")
+        rmat = const.tile([P, OUT], BF16, name="rmat")
+        nc.vector.memset(lmat[:], 0.0)
+        nc.vector.memset(lmat[32:64, :], -1.0)
+        nc.vector.memset(rmat[:], 0.0)
+        nc.scalar.dma_start(out=lmat[0:1, :], in_=lr_samples.rearrange("(a b) -> a b", a=1))
+        nc.scalar.dma_start(out=rmat[0:1, :], in_=prev_bias_grad.rearrange("(a b) -> a b", a=1))
+        nc.scalar.dma_start(out=rmat[32:33, :], in_=bias.rearrange("(a b) -> a b", a=1))
+        lrb = const.tile([P, NB], BF16, name="lrb")
+        with nc.allow_non_contiguous_dma(reason="lr, one value to a partition"):
+            nc.scalar.dma_start(out=lrb[:], in_=lr_samples.rearrange("(i p) -> p i", p=P))
+        for n in range(LOAD_AHEAD):
+            load()
+        ident = const.tile([P, P], F32, name="ident")
+        make_identity(nc, ident[:])
+        lrc = const.tile([P, NB], F32, name="lrc")
+        warm = const.tile([P, 1], F32, name="warm")
+        nc.vector.memset(warm[:], 0.0)
+        warm2 = const.tile([P, 1], F32, name="warm2")
+        nc.scalar.activation(out=warm2[:], in_=warm[:], func=ACT.Copy, scale=1.0)
+        nc.vector.tensor_copy(out=lrc[:], in_=lrb[:])
+        dsb = const.tile([P, NB, OUT], F32, name="dsb")
+        xcod = const.tile([P, PASSES * B], U32, name="xcod", align_bytes=64)
+        xscl = const.tile([P, PASSES * B], U8, name="xscl", align_bytes=64)
+        cod[0] = (xcod, xscl)
+
+        def deint_tile(u, rt):
+            mode = DEI.get((u, rt), DEI_DEFAULT)
+            if mode == "n":
+                return
+            d = deip.tile([P, PASSES, 2, P], F32, name="dei")
+            dei[(u, rt)] = d
+            src = raw[(u, rt)][:].bitcast(F32).rearrange("p (g j w) -> p g w j", g=PASSES, w=2)
+            if mode == "v":
+                nc.vector.tensor_copy(out=d[:], in_=src)
+            else:
+                nc.scalar.copy(out=d[:], in_=src)
+            freed.add((u, rt))
+
+        def deint_list(k):
+            if k >= NT:
+                return []
+            u, part = truns[k]
+            rows = units[u][2]
+            if rows == 512:
+                return [(u, rt) for rt in range(4)] if part == 0 else []
+            return [(u, 0), (u, 1)]
+
+        def trun(k):
+            u, part = truns[k]
+            rows = units[u][2]
+            eng = CO.get(k, CO_DEFAULT)
+            ng = 1024 // rows
+            g_tile = grpp.tile([P, 4096], BF16, name="grp", align_bytes=64)
+            grp[k] = g_tile
+            gview = g_tile[:].bitcast(F32).rearrange("p (g o w) -> p g o w", g=ng, w=2)
+            n = 0
+            for rt in range(rows // P):
+                for half in range(ng // 2):
+                    bank = tpp.tile([P, 4, P], F32, name="bank")
+                    for g2 in range(2):
+                        g = (2 * part if rows == 512 else 2 * half) + g2
+                        for w in range(2):
+                            if (u, rt) in dei:
+                                src = dei[(u, rt)][:, g, w, :]
+                            else:
+                                src = raw[(u, rt)][:].bitcast(F32)[:, 256 * g + w:256 * (g + 1):2]
+                            nc.tensor.transpose(bank[:, 2 * g2 + w, :], src, ident[:])
+                    dst = gview[:, 2 * half:2 * half + 2, rt * P:(rt + 1) * P, :]
+                    srcb = bank[:].rearrange("p (g w) r -> p g r w", w=2)
+                    if eng[n] == "s":
+                        nc.scalar.copy(out=dst, in_=srcb)
+                    else:
+                        nc.vector.tensor_copy(out=dst, in_=srcb)
+                    n += 1
+            if k + 1 >= NT or truns[k + 1][0] != u:
+                for rt in range(rows // P):
+                    freed.add((u, rt))
+                state["used"] += rows // P
+
+        def quant(k):
+            u, part = truns[k]
+            rows = units[u][2]
+            if u not in cod:
+                tag = "w" if u % 2 == 1 else "g"
+                cc = codp.tile([P, PASSES * 512], U32, name=tag + "cod", align_bytes=64)
+                ss = codp.tile([P, PASSES * 512], U8, name=tag + "scl", align_bytes=64)
+                cod[u] = (cc, ss)
+            cc, ss = cod[u]
+            sl = slice(part * 1024, (part + 1) * 1024)
+            nc.vector.quantize_mx(out=cc[:, sl].bitcast(FP8X4), scales=ss[:, sl], in_=grp[k][:])
+
+        def dmm(c, i):
+            wdt = CHUNKS[c]
+            cols = slice(starts[c], starts[c] + wdt)
+            dps = accp.tile([P, 512], F32, name="acc")
+            nc.tensor.matmul(out=dps[:, 0:wdt], lhsT=lmat[:, i * P:(i + 1) * P], rhs=rmat[:, cols], start=True, stop=True)
+            if DEV[state["nd"] % len(DEV)] == "s":
+                nc.scalar.copy(out=dsb[:, i, cols], in_=dps[:, 0:wdt])
+            else:
+                nc.vector.tensor_copy(out=dsb[:, i, cols], in_=dps[:, 0:wdt])
+            state["nd"] += 1
+
+        def mrun(j):
+            for (c, i) in mruns[j]:
+                wdt = CHUNKS[c]
+                if wdt == 512:
+                    a0 = accp.tile([P, 512], F32, name="acc")
+                    a1 = accp.tile([P, 512], F32, name="acc")
+                    outs = [a0[:], a1[:]]
+                else:
+                    bk = accp.tile([P, 512], F32, name="acc")
+                    outs = [bk[:, 0:256], bk[:, 256:512]]
+                acc[(c, i)] = outs
+                for m in (1, 0):
+                    cc, ss = cod[1 + 2 * c + m]
+                    for g in range(PASSES):
+                        xs = slice(g * B + i * P, g * B + (i + 1) * P)
+                        ws = slice(g * wdt, (g + 1) * wdt)
+                        nc.tensor.matmul_mx(out=outs[m], lhsT=xcod[:, xs].bitcast(FP8X4), lhsT_scale=xscl[:, xs],
+                                            rhs=cc[:, ws].bitcast(FP8X4), rhs_scale=ss[:, ws],
+                                            start=(g == 0), stop=(g == PASSES - 1))
+
+        def epi_a(j):
+            for (c, i) in mruns[j]:
+                wdt = CHUNKS[c]
+                cols = slice(starts[c], starts[c] + wdt)
+                t = epp.tile([P, 512], F32, name="t")
+                tmp[(c, i)] = t
+                nc.vector.scalar_tensor_tensor(out=t[:, 0:wdt], in0=acc[(c, i)][1], scalar=lrc[:, i:i + 1], in1=dsb[:, i, cols],
+                                               op0=ALU.mult, op1=ALU.add)
+
+        def epi_b(j):
+            for (c, i) in mruns[j]:
+                wdt = CHUNKS[c]
+                cols = slice(starts[c], starts[c] + wdt)
+                rws = slice(i * P, (i + 1) * P)
+                o = epp.tile([P, 512], F32, name="o")
+                nc.vector.tensor_tensor(out=o[:, 0:wdt], in0=acc[(c, i)][0], in1=tmp[(c, i)][:, 0:wdt], op=ALU.subtract)
+                f8 = epp.tile([P, 512], FP8, name="f8")
+                if CAST_ON == "s":
+                    nc.scalar.activation(out=f8[:, 0:wdt], in_=o[:, 0:wdt], func=ACT.Copy, scale=Y_SCALE, saturate=False)
+                else:
+                    nc.vector.tensor_scalar(out=f8[:, 0:wdt], in0=o[:, 0:wdt], scalar1=Y_SCALE, scalar2=None, op0=ALU.mult, saturate=False)
+                nc.sync.dma_start(out=out_0[rws, cols], in_=o[:, 0:wdt])
+                nc.sync.dma_start(out=out_1[rws, cols], in_=f8[:, 0:wdt].bitcast(U8))
+
+        dq = []
+        for k in range(DEI_AHEAD):
+            dq.extend(deint_list(k))
+        for (u, rt) in dq:
+            deint_tile(u, rt)
+        dq = []
+        pend_q = []
+        pend_e = []
+        for item in seq:
+            if item[0] == "D":
+                dmm(item[1], item[2])
+                continue
+            new_q = []
+            new_e = []
+            if item[0] == "T":
+                k = item[1]
+                for n in range(4):
+                    load()
+                dq.extend(deint_list(k + DEI_AHEAD))
+                trun(k)
+                new_q.append(k)
+            else:
+                mrun(item[1])
+                new_e.append(item[1])
+            for k in pend_q:
+                quant(k)
+            for j in pend_e:
+                epi_a(j)
+            if item[0] == "T":
+                for (u, rt) in dq[:1]:
+                    deint_tile(u, rt)
+                dq = dq[1:]
+            for j in pend_e:
+                epi_b(j)
+            if item[0] == "T":
+                for (u, rt) in dq[:1]:
+                    deint_tile(u, rt)
+                dq = dq[1:]
+            pend_q = new_q
+            pend_e = new_e
+        for j in pend_e:
+            epi_a(j)
+            epi_b(j)

@@ -19,63 +19,38 @@ ACT = mybir.ActivationFunctionType
 P = 128
 PASSES = IN // 512
 NB = B // P
+CW = 256
+NC = OUT // CW
 
-CHUNKS = (256, 256, 512, 512, 512)
-DEI_DEFAULT = "n"
-DEI = {}
-CO_DEFAULT = "ssss"
-CO = {}
-DEV = "sv"
+DEI_FROM = 4
+DEI_PATTERN = "vv"
+CO = "ssss"
+DEV = "ss"
 RAW_BUFS = 12
-DEI_BUFS = 8
-LOAD_AHEAD = 12
-DEI_AHEAD = 2
-D_FIRST = 8
-D_PER_T = 2
+DEI_BUFS = 6
+COD_BUFS = 4
+LEAD = 5
 CAST_ON = "s"
-LEADS = (5, 7, 9, 11)
-LEAD_STEADY = 8
+STORE_ON = "s"
 
 
 def tile_optimizedlinear_kernel(tc, input_data, weight, bias, prev_grad, prev_bias_grad, lr_samples, out_0, out_1):
     nc = tc.nc
-    starts = [sum(CHUNKS[:c]) for c in range(len(CHUNKS))]
 
-    units = [(input_data, 0, B)]
-    for c, wdt in enumerate(CHUNKS):
-        units.append((weight, starts[c], wdt))
-        units.append((prev_grad, starts[c], wdt))
-    tiles = [(u, rt) for u in range(len(units)) for rt in range(units[u][2] // P)]
-    truns = [(u, part) for u in range(len(units)) for part in range(units[u][2] // 256)]
-    NT = len(truns)
-    mruns = []
-    for c, wdt in enumerate(CHUNKS):
-        per = 512 // wdt
-        for i0 in range(0, NB, per):
-            mruns.append([(c, i) for i in range(i0, i0 + per)])
-    NM = len(mruns)
-    ditems = [(c, i) for c in range(len(CHUNKS)) for i in range(NB)]
-
-    seq = [("D", c, i) for (c, i) in ditems[:D_FIRST]]
-    dleft = ditems[D_FIRST:]
-    done_t = 0
-    for j in range(NM):
-        want = LEADS[j] if j < len(LEADS) else min(NT, LEAD_STEADY + j)
-        while done_t < want:
-            seq.append(("T", done_t))
-            done_t += 1
-            for (c, i) in dleft[:D_PER_T]:
-                seq.append(("D", c, i))
-            dleft = dleft[D_PER_T:]
-        seq.append(("M", j))
+    units = [("x", 0, input_data, 0), ("w", 0, weight, 0), ("g", 0, prev_grad, 0), ("x", 1, input_data, CW)]
+    for c in range(1, NC):
+        units.append(("w", c, weight, c * CW))
+        units.append(("g", c, prev_grad, c * CW))
+    NU = len(units)
+    NM = 2 * NC
 
     with ExitStack() as ctx:
         const = ctx.enter_context(tc.tile_pool(name="const", bufs=1))
         rawp = ctx.enter_context(tc.tile_pool(name="rawp", bufs=RAW_BUFS))
         deip = ctx.enter_context(tc.tile_pool(name="deip", bufs=DEI_BUFS))
         grpp = ctx.enter_context(tc.tile_pool(name="grpp", bufs=3))
-        codp = ctx.enter_context(tc.tile_pool(name="codp", bufs=3))
-        epp = ctx.enter_context(tc.tile_pool(name="epp", bufs=3))
+        codp = ctx.enter_context(tc.tile_pool(name="codp", bufs=COD_BUFS))
+        epp = ctx.enter_context(tc.tile_pool(name="epp", bufs=4))
         tpp = ctx.enter_context(tc.psum_pool(name="tpp", bufs=4))
         accp = ctx.enter_context(tc.psum_pool(name="accp", bufs=4))
         ctx.enter_context(tc.manual_schedule())
@@ -86,36 +61,32 @@ def tile_optimizedlinear_kernel(tc, input_data, weight, bias, prev_grad, prev_bi
         cod = {}
         acc = {}
         tmp = {}
-        state = {"loaded": 0, "used": 0, "nd": 0}
-
-        freed = set()
+        state = {"loaded": 0, "freed": 0}
 
         def load():
             n = state["loaded"]
-            if n >= len(tiles) or n - state["used"] >= LOAD_AHEAD:
+            if n >= 2 * NU or n - state["freed"] >= RAW_BUFS:
                 return
-            if n >= RAW_BUFS and tiles[n - RAW_BUFS] not in freed:
-                return
-            u, rt = tiles[n]
             state["loaded"] += 1
-            src, r0, rows = units[u]
+            kind, idx, src, r0 = units[n // 2]
             tl = rawp.tile([P, IN], BF16, name="raw")
-            raw[(u, rt)] = tl
-            nc.sync.dma_start(out=tl[:], in_=src[r0 + rt * P:r0 + (rt + 1) * P, :])
+            raw[n] = tl
+            nc.sync.dma_start(out=tl[:], in_=src[r0 + (n % 2) * P:r0 + (n % 2 + 1) * P, :])
 
+        stage = const.tile([P, OUT + B], BF16, name="stage")
+        lrb = const.tile([P, NB], BF16, name="lrb")
+        nc.sync.dma_start(out=stage[0:1, 0:OUT], in_=prev_bias_grad.rearrange("(a b) -> a b", a=1))
+        nc.sync.dma_start(out=stage[32:33, 0:OUT], in_=bias.rearrange("(a b) -> a b", a=1))
+        nc.sync.dma_start(out=stage[0:1, OUT:OUT + B], in_=lr_samples.rearrange("(a b) -> a b", a=1))
+        with nc.allow_non_contiguous_dma(reason="lr, one value to a partition"):
+            nc.scalar.dma_start(out=lrb[:], in_=lr_samples.rearrange("(i p) -> p i", p=P))
+        for n in range(RAW_BUFS):
+            load()
         lmat = const.tile([P, B], BF16, name="lmat")
         rmat = const.tile([P, OUT], BF16, name="rmat")
         nc.vector.memset(lmat[:], 0.0)
         nc.vector.memset(lmat[32:64, :], -1.0)
         nc.vector.memset(rmat[:], 0.0)
-        nc.scalar.dma_start(out=lmat[0:1, :], in_=lr_samples.rearrange("(a b) -> a b", a=1))
-        nc.scalar.dma_start(out=rmat[0:1, :], in_=prev_bias_grad.rearrange("(a b) -> a b", a=1))
-        nc.scalar.dma_start(out=rmat[32:33, :], in_=bias.rearrange("(a b) -> a b", a=1))
-        lrb = const.tile([P, NB], BF16, name="lrb")
-        with nc.allow_non_contiguous_dma(reason="lr, one value to a partition"):
-            nc.scalar.dma_start(out=lrb[:], in_=lr_samples.rearrange("(i p) -> p i", p=P))
-        for n in range(LOAD_AHEAD):
-            load()
         ident = const.tile([P, P], F32, name="ident")
         make_identity(nc, ident[:])
         lrc = const.tile([P, NB], F32, name="lrc")
@@ -123,173 +94,130 @@ def tile_optimizedlinear_kernel(tc, input_data, weight, bias, prev_grad, prev_bi
         nc.vector.memset(warm[:], 0.0)
         warm2 = const.tile([P, 1], F32, name="warm2")
         nc.scalar.activation(out=warm2[:], in_=warm[:], func=ACT.Copy, scale=1.0)
+        nc.vector.tensor_copy(out=lmat[0:1, :], in_=stage[0:1, OUT:OUT + B])
+        nc.vector.tensor_copy(out=rmat[0:1, :], in_=stage[0:1, 0:OUT])
+        nc.vector.tensor_copy(out=rmat[32:33, :], in_=stage[32:33, 0:OUT])
         nc.vector.tensor_copy(out=lrc[:], in_=lrb[:])
         dsb = const.tile([P, NB, OUT], F32, name="dsb")
-        xcod = const.tile([P, PASSES * B], U32, name="xcod", align_bytes=64)
-        xscl = const.tile([P, PASSES * B], U8, name="xscl", align_bytes=64)
-        cod[0] = (xcod, xscl)
 
-        def deint_tile(u, rt):
-            mode = DEI.get((u, rt), DEI_DEFAULT)
-            if mode == "n":
+        def deint(u, t):
+            if u >= NU or u < DEI_FROM:
                 return
             d = deip.tile([P, PASSES, 2, P], F32, name="dei")
-            dei[(u, rt)] = d
-            src = raw[(u, rt)][:].bitcast(F32).rearrange("p (g j w) -> p g w j", g=PASSES, w=2)
-            if mode == "v":
+            dei[2 * u + t] = d
+            src = raw[2 * u + t][:].bitcast(F32).rearrange("p (g j w) -> p g w j", g=PASSES, w=2)
+            if DEI_PATTERN[t] == "v":
                 nc.vector.tensor_copy(out=d[:], in_=src)
             else:
                 nc.scalar.copy(out=d[:], in_=src)
-            freed.add((u, rt))
 
-        def deint_list(k):
-            if k >= NT:
-                return []
-            u, part = truns[k]
-            rows = units[u][2]
-            if rows == 512:
-                return [(u, rt) for rt in range(4)] if part == 0 else []
-            return [(u, 0), (u, 1)]
-
-        def trun(k):
-            u, part = truns[k]
-            rows = units[u][2]
-            eng = CO.get(k, CO_DEFAULT)
-            ng = 1024 // rows
+        def trun(u):
             g_tile = grpp.tile([P, 4096], BF16, name="grp", align_bytes=64)
-            grp[k] = g_tile
-            gview = g_tile[:].bitcast(F32).rearrange("p (g o w) -> p g o w", g=ng, w=2)
-            n = 0
-            for rt in range(rows // P):
-                for half in range(ng // 2):
+            grp[u] = g_tile
+            gview = g_tile[:].bitcast(F32).rearrange("p (g o w) -> p g o w", g=PASSES, w=2)
+            for t in range(2):
+                for half in range(2):
                     bank = tpp.tile([P, 4, P], F32, name="bank")
                     for g2 in range(2):
-                        g = (2 * part if rows == 512 else 2 * half) + g2
+                        g = 2 * half + g2
                         for w in range(2):
-                            if (u, rt) in dei:
-                                src = dei[(u, rt)][:, g, w, :]
+                            if 2 * u + t in dei:
+                                src = dei[2 * u + t][:, g, w, :]
                             else:
-                                src = raw[(u, rt)][:].bitcast(F32)[:, 256 * g + w:256 * (g + 1):2]
+                                src = raw[2 * u + t][:].bitcast(F32)[:, 256 * g + w:256 * (g + 1):2]
                             nc.tensor.transpose(bank[:, 2 * g2 + w, :], src, ident[:])
-                    dst = gview[:, 2 * half:2 * half + 2, rt * P:(rt + 1) * P, :]
+                    dst = gview[:, 2 * half:2 * half + 2, t * P:(t + 1) * P, :]
                     srcb = bank[:].rearrange("p (g w) r -> p g r w", w=2)
-                    if eng[n] == "s":
+                    if CO[2 * t + half] == "s":
                         nc.scalar.copy(out=dst, in_=srcb)
                     else:
                         nc.vector.tensor_copy(out=dst, in_=srcb)
-                    n += 1
-            if k + 1 >= NT or truns[k + 1][0] != u:
-                for rt in range(rows // P):
-                    freed.add((u, rt))
-                state["used"] += rows // P
+            state["freed"] = 2 * u + 2
 
-        def quant(k):
-            u, part = truns[k]
-            rows = units[u][2]
-            if u not in cod:
-                tag = "w" if u % 2 == 1 else "g"
-                cc = codp.tile([P, PASSES * 512], U32, name=tag + "cod", align_bytes=64)
-                ss = codp.tile([P, PASSES * 512], U8, name=tag + "scl", align_bytes=64)
-                cod[u] = (cc, ss)
-            cc, ss = cod[u]
-            sl = slice(part * 1024, (part + 1) * 1024)
-            nc.vector.quantize_mx(out=cc[:, sl].bitcast(FP8X4), scales=ss[:, sl], in_=grp[k][:])
+        def quant(u):
+            kind, idx = units[u][0], units[u][1]
+            nbufs = 2 if kind == "x" else COD_BUFS
+            cc = codp.tile([P, PASSES * CW], U32, name=kind + "cod", bufs=nbufs, align_bytes=64)
+            ss = codp.tile([P, PASSES * CW], U8, name=kind + "scl", bufs=nbufs, align_bytes=64)
+            cod[(kind, idx)] = (cc, ss)
+            nc.vector.quantize_mx(out=cc[:].bitcast(FP8X4), scales=ss[:], in_=grp[u][:])
 
-        def dmm(c, i):
-            wdt = CHUNKS[c]
-            cols = slice(starts[c], starts[c] + wdt)
-            dps = accp.tile([P, 512], F32, name="acc")
-            nc.tensor.matmul(out=dps[:, 0:wdt], lhsT=lmat[:, i * P:(i + 1) * P], rhs=rmat[:, cols], start=True, stop=True)
-            if DEV[state["nd"] % len(DEV)] == "s":
-                nc.scalar.copy(out=dsb[:, i, cols], in_=dps[:, 0:wdt])
+        def dmm(n, eng):
+            if n >= NC * NB // 2:
+                return
+            c, i = n // 2, 2 * (n % 2)
+            cols = slice(c * CW, (c + 1) * CW)
+            dps = tpp.tile([P, 2, CW], F32, name="bank")
+            for q in range(2):
+                nc.tensor.matmul(out=dps[:, q, :], lhsT=lmat[:, (i + q) * P:(i + q + 1) * P], rhs=rmat[:, cols], start=True, stop=True)
+            if eng == "s":
+                nc.scalar.copy(out=dsb[:, i:i + 2, cols], in_=dps[:])
             else:
-                nc.vector.tensor_copy(out=dsb[:, i, cols], in_=dps[:, 0:wdt])
-            state["nd"] += 1
+                nc.vector.tensor_copy(out=dsb[:, i:i + 2, cols], in_=dps[:])
 
         def mrun(j):
-            for (c, i) in mruns[j]:
-                wdt = CHUNKS[c]
-                if wdt == 512:
-                    a0 = accp.tile([P, 512], F32, name="acc")
-                    a1 = accp.tile([P, 512], F32, name="acc")
-                    outs = [a0[:], a1[:]]
-                else:
-                    bk = accp.tile([P, 512], F32, name="acc")
-                    outs = [bk[:, 0:256], bk[:, 256:512]]
-                acc[(c, i)] = outs
+            c, h = j // 2, j % 2
+            xc, xs = cod[("x", h)]
+            for t in range(2):
+                bk = accp.tile([P, 2, CW], F32, name="acc")
+                acc[(j, t)] = bk
                 for m in (1, 0):
-                    cc, ss = cod[1 + 2 * c + m]
+                    cc, ss = cod[("wg"[m], c)]
                     for g in range(PASSES):
-                        xs = slice(g * B + i * P, g * B + (i + 1) * P)
-                        ws = slice(g * wdt, (g + 1) * wdt)
-                        nc.tensor.matmul_mx(out=outs[m], lhsT=xcod[:, xs].bitcast(FP8X4), lhsT_scale=xscl[:, xs],
+                        xsl = slice(g * CW + t * P, g * CW + (t + 1) * P)
+                        ws = slice(g * CW, (g + 1) * CW)
+                        nc.tensor.matmul_mx(out=bk[:, m, :], lhsT=xc[:, xsl].bitcast(FP8X4), lhsT_scale=xs[:, xsl],
                                             rhs=cc[:, ws].bitcast(FP8X4), rhs_scale=ss[:, ws],
                                             start=(g == 0), stop=(g == PASSES - 1))
 
         def epi_a(j):
-            for (c, i) in mruns[j]:
-                wdt = CHUNKS[c]
-                cols = slice(starts[c], starts[c] + wdt)
-                t = epp.tile([P, 512], F32, name="t")
-                tmp[(c, i)] = t
-                nc.vector.scalar_tensor_tensor(out=t[:, 0:wdt], in0=acc[(c, i)][1], scalar=lrc[:, i:i + 1], in1=dsb[:, i, cols],
-                                               op0=ALU.mult, op1=ALU.add)
+            c, h = j // 2, j % 2
+            for t in range(2):
+                i = 2 * h + t
+                tt = epp.tile([P, CW], F32, name="t")
+                tmp[(j, t)] = tt
+                nc.vector.scalar_tensor_tensor(out=tt[:], in0=acc[(j, t)][:, 1, :], scalar=lrc[:, i:i + 1],
+                                               in1=dsb[:, i, c * CW:(c + 1) * CW], op0=ALU.mult, op1=ALU.add)
 
         def epi_b(j):
-            for (c, i) in mruns[j]:
-                wdt = CHUNKS[c]
-                cols = slice(starts[c], starts[c] + wdt)
+            c, h = j // 2, j % 2
+            cols = slice(c * CW, (c + 1) * CW)
+            for t in range(2):
+                i = 2 * h + t
                 rws = slice(i * P, (i + 1) * P)
-                o = epp.tile([P, 512], F32, name="o")
-                nc.vector.tensor_tensor(out=o[:, 0:wdt], in0=acc[(c, i)][0], in1=tmp[(c, i)][:, 0:wdt], op=ALU.subtract)
-                f8 = epp.tile([P, 512], FP8, name="f8")
+                o = epp.tile([P, CW], F32, name="o", bufs=8)
+                nc.vector.tensor_tensor(out=o[:], in0=acc[(j, t)][:, 0, :], in1=tmp[(j, t)][:], op=ALU.subtract)
+                f8 = epp.tile([P, CW], FP8, name="f8", bufs=12)
                 if CAST_ON == "s":
-                    nc.scalar.activation(out=f8[:, 0:wdt], in_=o[:, 0:wdt], func=ACT.Copy, scale=Y_SCALE, saturate=False)
+                    nc.scalar.activation(out=f8[:], in_=o[:], func=ACT.Copy, scale=Y_SCALE, saturate=False)
                 else:
-                    nc.vector.tensor_scalar(out=f8[:, 0:wdt], in0=o[:, 0:wdt], scalar1=Y_SCALE, scalar2=None, op0=ALU.mult, saturate=False)
-                nc.sync.dma_start(out=out_0[rws, cols], in_=o[:, 0:wdt])
-                nc.sync.dma_start(out=out_1[rws, cols], in_=f8[:, 0:wdt].bitcast(U8))
+                    nc.vector.tensor_scalar(out=f8[:], in0=o[:], scalar1=Y_SCALE, scalar2=None, op0=ALU.mult, saturate=False)
+                if STORE_ON == "s":
+                    nc.scalar.dma_start(out=out_0[rws, cols], in_=o[:])
+                else:
+                    nc.sync.dma_start(out=out_0[rws, cols], in_=o[:])
+                nc.sync.dma_start(out=out_1[rws, cols], in_=f8[:].bitcast(U8))
 
-        dq = []
-        for k in range(DEI_AHEAD):
-            dq.extend(deint_list(k))
-        for (u, rt) in dq:
-            deint_tile(u, rt)
-        dq = []
-        pend_q = []
-        pend_e = []
-        for item in seq:
-            if item[0] == "D":
-                dmm(item[1], item[2])
-                continue
-            new_q = []
-            new_e = []
-            if item[0] == "T":
-                k = item[1]
-                for n in range(4):
-                    load()
-                dq.extend(deint_list(k + DEI_AHEAD))
-                trun(k)
-                new_q.append(k)
-            else:
-                mrun(item[1])
-                new_e.append(item[1])
-            for k in pend_q:
-                quant(k)
-            for j in pend_e:
-                epi_a(j)
-            if item[0] == "T":
-                for (u, rt) in dq[:1]:
-                    deint_tile(u, rt)
-                dq = dq[1:]
-            for j in pend_e:
-                epi_b(j)
-            if item[0] == "T":
-                for (u, rt) in dq[:1]:
-                    deint_tile(u, rt)
-                dq = dq[1:]
-            pend_q = new_q
-            pend_e = new_e
-        for j in pend_e:
-            epi_a(j)
-            epi_b(j)
+        deint(0, 0)
+        deint(0, 1)
+        for s in range(NM + LEAD - 1):
+            j = s - LEAD + 1 if s >= LEAD else (0 if s == 3 else -1)
+            if s == LEAD - 1 and LEAD > 4:
+                j = -1
+            if s < NU:
+                trun(s)
+                dmm(s, DEV[s % 2])
+                load()
+                load()
+            if 1 <= s <= NU:
+                quant(s - 1)
+            if j >= 0:
+                mrun(j)
+            if j >= 1:
+                epi_a(j - 1)
+            deint(s + 1, 0)
+            if j >= 1:
+                epi_b(j - 1)
+            deint(s + 1, 1)
+        epi_a(NM - 1)
+        epi_b(NM - 1)

@@ -32,6 +32,8 @@ COD_BUFS = 4
 LEAD = 5
 CAST_ON = "s"
 STORE_ON = "s"
+FIRST_SPLIT = 2
+N_WARM = 6
 
 
 def tile_optimizedlinear_kernel(tc, input_data, weight, bias, prev_grad, prev_bias_grad, lr_samples, out_0, out_1):
@@ -71,17 +73,26 @@ def tile_optimizedlinear_kernel(tc, input_data, weight, bias, prev_grad, prev_bi
             kind, idx, src, r0 = units[n // 2]
             tl = rawp.tile([P, IN], BF16, name="raw")
             raw[n] = tl
-            nc.sync.dma_start(out=tl[:], in_=src[r0 + (n % 2) * P:r0 + (n % 2 + 1) * P, :])
+            rows = slice(r0 + (n % 2) * P, r0 + (n % 2 + 1) * P)
+            pieces = FIRST_SPLIT if n == 0 else 1
+            for q in range(pieces):
+                cs = slice(q * IN // pieces, (q + 1) * IN // pieces)
+                nc.sync.dma_start(out=tl[:, cs], in_=src[rows, cs])
 
         stage = const.tile([P, OUT + B], BF16, name="stage")
         lrb = const.tile([P, NB], BF16, name="lrb")
-        nc.sync.dma_start(out=stage[0:1, 0:OUT], in_=prev_bias_grad.rearrange("(a b) -> a b", a=1))
-        nc.sync.dma_start(out=stage[32:33, 0:OUT], in_=bias.rearrange("(a b) -> a b", a=1))
-        nc.sync.dma_start(out=stage[0:1, OUT:OUT + B], in_=lr_samples.rearrange("(a b) -> a b", a=1))
+        nc.scalar.dma_start(out=stage[0:1, 0:OUT], in_=prev_bias_grad.rearrange("(a b) -> a b", a=1))
+        nc.scalar.dma_start(out=stage[32:33, 0:OUT], in_=bias.rearrange("(a b) -> a b", a=1))
+        nc.scalar.dma_start(out=stage[0:1, OUT:OUT + B], in_=lr_samples.rearrange("(a b) -> a b", a=1))
         with nc.allow_non_contiguous_dma(reason="lr, one value to a partition"):
             nc.scalar.dma_start(out=lrb[:], in_=lr_samples.rearrange("(i p) -> p i", p=P))
         for n in range(RAW_BUFS):
             load()
+        wz = const.tile([P, 512], BF16, name="wz")
+        nc.vector.memset(wz[:], 0.0)
+        for n in range(N_WARM):
+            wps = tpp.tile([P, 512], F32, name="bank")
+            nc.tensor.matmul(out=wps[:], lhsT=wz[:, 0:P], rhs=wz[:], start=True, stop=True)
         lmat = const.tile([P, B], BF16, name="lmat")
         rmat = const.tile([P, OUT], BF16, name="rmat")
         nc.vector.memset(lmat[:], 0.0)
@@ -98,7 +109,7 @@ def tile_optimizedlinear_kernel(tc, input_data, weight, bias, prev_grad, prev_bi
         nc.vector.tensor_copy(out=rmat[0:1, :], in_=stage[0:1, 0:OUT])
         nc.vector.tensor_copy(out=rmat[32:33, :], in_=stage[32:33, 0:OUT])
         nc.vector.tensor_copy(out=lrc[:], in_=lrb[:])
-        dsb = const.tile([P, NB, OUT], F32, name="dsb")
+        dsb = const.tile([P, NC, NB, CW], F32, name="dsb")
 
         def deint(u, t):
             if u >= NU or u < DEI_FROM:
@@ -151,24 +162,31 @@ def tile_optimizedlinear_kernel(tc, input_data, weight, bias, prev_grad, prev_bi
             for q in range(2):
                 nc.tensor.matmul(out=dps[:, q, :], lhsT=lmat[:, (i + q) * P:(i + q + 1) * P], rhs=rmat[:, cols], start=True, stop=True)
             if eng == "s":
-                nc.scalar.copy(out=dsb[:, i:i + 2, cols], in_=dps[:])
+                nc.scalar.copy(out=dsb[:, c, i:i + 2, :], in_=dps[:])
             else:
-                nc.vector.tensor_copy(out=dsb[:, i:i + 2, cols], in_=dps[:])
+                nc.vector.tensor_copy(out=dsb[:, c, i:i + 2, :], in_=dps[:])
 
         def mrun(j):
             c, h = j // 2, j % 2
             xc, xs = cod[("x", h)]
+            last = j == NM - 1
             for t in range(2):
-                bk = accp.tile([P, 2, CW], F32, name="acc")
-                acc[(j, t)] = bk
-                for m in (1, 0):
-                    cc, ss = cod[("wg"[m], c)]
-                    for g in range(PASSES):
-                        xsl = slice(g * CW + t * P, g * CW + (t + 1) * P)
-                        ws = slice(g * CW, (g + 1) * CW)
-                        nc.tensor.matmul_mx(out=bk[:, m, :], lhsT=xc[:, xsl].bitcast(FP8X4), lhsT_scale=xs[:, xsl],
-                                            rhs=cc[:, ws].bitcast(FP8X4), rhs_scale=ss[:, ws],
-                                            start=(g == 0), stop=(g == PASSES - 1))
+                if last:
+                    pbk = tpp.tile([P, CW], F32, name="bank")
+                    bbk = accp.tile([P, CW], F32, name="acc")
+                    acc[(j, t)] = [bbk[:], pbk[:]]
+                else:
+                    bk = accp.tile([P, 2, CW], F32, name="acc")
+                    acc[(j, t)] = [bk[:, 0, :], bk[:, 1, :]]
+            order = [(1, 0), (1, 1), (0, 0), (0, 1)] if last else [(1, 0), (0, 0), (1, 1), (0, 1)]
+            for (m, t) in order:
+                cc, ss = cod[("wg"[m], c)]
+                for g in range(PASSES):
+                    xsl = slice(g * CW + t * P, g * CW + (t + 1) * P)
+                    ws = slice(g * CW, (g + 1) * CW)
+                    nc.tensor.matmul_mx(out=acc[(j, t)][m], lhsT=xc[:, xsl].bitcast(FP8X4), lhsT_scale=xs[:, xsl],
+                                        rhs=cc[:, ws].bitcast(FP8X4), rhs_scale=ss[:, ws],
+                                        start=(g == 0), stop=(g == PASSES - 1))
 
         def epi_a(j):
             c, h = j // 2, j % 2
@@ -176,8 +194,8 @@ def tile_optimizedlinear_kernel(tc, input_data, weight, bias, prev_grad, prev_bi
                 i = 2 * h + t
                 tt = epp.tile([P, CW], F32, name="t")
                 tmp[(j, t)] = tt
-                nc.vector.scalar_tensor_tensor(out=tt[:], in0=acc[(j, t)][:, 1, :], scalar=lrc[:, i:i + 1],
-                                               in1=dsb[:, i, c * CW:(c + 1) * CW], op0=ALU.mult, op1=ALU.add)
+                nc.vector.scalar_tensor_tensor(out=tt[:], in0=acc[(j, t)][1], scalar=lrc[:, i:i + 1],
+                                               in1=dsb[:, c, i, :], op0=ALU.mult, op1=ALU.add)
 
         def epi_b(j):
             c, h = j // 2, j % 2
@@ -186,7 +204,7 @@ def tile_optimizedlinear_kernel(tc, input_data, weight, bias, prev_grad, prev_bi
                 i = 2 * h + t
                 rws = slice(i * P, (i + 1) * P)
                 o = epp.tile([P, CW], F32, name="o", bufs=8)
-                nc.vector.tensor_tensor(out=o[:], in0=acc[(j, t)][:, 0, :], in1=tmp[(j, t)][:], op=ALU.subtract)
+                nc.vector.tensor_tensor(out=o[:], in0=acc[(j, t)][0], in1=tmp[(j, t)][:], op=ALU.subtract)
                 f8 = epp.tile([P, CW], FP8, name="f8", bufs=12)
                 if CAST_ON == "s":
                     nc.scalar.activation(out=f8[:], in_=o[:], func=ACT.Copy, scale=Y_SCALE, saturate=False)

@@ -19,32 +19,46 @@ ACT = mybir.ActivationFunctionType
 P = 128
 PASSES = IN // 512
 NB = B // P
-CW = 256
+UR = 256
+CW = 512
 NC = OUT // CW
 
-DEI_FROM = 4
-DEI_PATTERN = "vv"
+DEI_FROM = 6
+DEI_ENG = "v"
 CO = "ssss"
-DEV = "ss"
-RAW_BUFS = 12
-DEI_BUFS = 6
+DEV_HEAD = "v"
+DEV = "s"
+RAW_BUFS = 6
+DEI_BUFS = 3
 COD_BUFS = 4
-LEAD = 5
-CAST_ON = "s"
 STORE_ON = "s"
-FIRST_SPLIT = 2
-N_WARM = 6
+EXTRA_T_BEFORE = 3
+DEI_AHEAD = 1
 
 
 def tile_optimizedlinear_kernel(tc, input_data, weight, bias, prev_grad, prev_bias_grad, lr_samples, out_0, out_1):
     nc = tc.nc
 
-    units = [("x", 0, input_data, 0), ("w", 0, weight, 0), ("g", 0, prev_grad, 0), ("x", 1, input_data, CW)]
-    for c in range(1, NC):
-        units.append(("w", c, weight, c * CW))
-        units.append(("g", c, prev_grad, c * CW))
+    units = [("x", 0, input_data, 0)]
+    for c in range(NC):
+        for h in range(2):
+            units.append(("w", 2 * c + h, weight, c * CW + h * UR))
+            units.append(("g", 2 * c + h, prev_grad, c * CW + h * UR))
+        if c == 0:
+            units.append(("x", 1, input_data, UR))
     NU = len(units)
-    NM = 2 * NC
+    NM = NC * NB
+
+    seq = [("T", u) for u in range(6)]
+    nxt = 6
+    for j in range(NM):
+        if j == EXTRA_T_BEFORE and nxt < NU:
+            seq.append(("T", nxt))
+            nxt += 1
+        seq.append(("M", j))
+        if nxt < NU:
+            seq.append(("T", nxt))
+            nxt += 1
 
     with ExitStack() as ctx:
         const = ctx.enter_context(tc.tile_pool(name="const", bufs=1))
@@ -52,7 +66,7 @@ def tile_optimizedlinear_kernel(tc, input_data, weight, bias, prev_grad, prev_bi
         deip = ctx.enter_context(tc.tile_pool(name="deip", bufs=DEI_BUFS))
         grpp = ctx.enter_context(tc.tile_pool(name="grpp", bufs=3))
         codp = ctx.enter_context(tc.tile_pool(name="codp", bufs=COD_BUFS))
-        epp = ctx.enter_context(tc.tile_pool(name="epp", bufs=4))
+        epp = ctx.enter_context(tc.tile_pool(name="epp", bufs=3))
         tpp = ctx.enter_context(tc.psum_pool(name="tpp", bufs=4))
         accp = ctx.enter_context(tc.psum_pool(name="accp", bufs=4))
         ctx.enter_context(tc.manual_schedule())
@@ -66,18 +80,15 @@ def tile_optimizedlinear_kernel(tc, input_data, weight, bias, prev_grad, prev_bi
         state = {"loaded": 0, "freed": 0}
 
         def load():
-            n = state["loaded"]
-            if n >= 2 * NU or n - state["freed"] >= RAW_BUFS:
+            u = state["loaded"]
+            if u >= NU or u - state["freed"] >= RAW_BUFS:
                 return
             state["loaded"] += 1
-            kind, idx, src, r0 = units[n // 2]
-            tl = rawp.tile([P, IN], BF16, name="raw")
-            raw[n] = tl
-            rows = slice(r0 + (n % 2) * P, r0 + (n % 2 + 1) * P)
-            pieces = FIRST_SPLIT if n == 0 else 1
-            for q in range(pieces):
-                cs = slice(q * IN // pieces, (q + 1) * IN // pieces)
-                nc.sync.dma_start(out=tl[:, cs], in_=src[rows, cs])
+            kind, idx, src, r0 = units[u]
+            tl = rawp.tile([P, 2, IN], BF16, name="raw")
+            raw[u] = tl
+            for t in range(2):
+                nc.sync.dma_start(out=tl[:, t, :], in_=src[r0 + t * P:r0 + (t + 1) * P, :])
 
         stage = const.tile([P, OUT + B], BF16, name="stage")
         lrb = const.tile([P, NB], BF16, name="lrb")
@@ -88,11 +99,6 @@ def tile_optimizedlinear_kernel(tc, input_data, weight, bias, prev_grad, prev_bi
             nc.scalar.dma_start(out=lrb[:], in_=lr_samples.rearrange("(i p) -> p i", p=P))
         for n in range(RAW_BUFS):
             load()
-        wz = const.tile([P, 512], BF16, name="wz")
-        nc.vector.memset(wz[:], 0.0)
-        for n in range(N_WARM):
-            wps = tpp.tile([P, 512], F32, name="bank")
-            nc.tensor.matmul(out=wps[:], lhsT=wz[:, 0:P], rhs=wz[:], start=True, stop=True)
         lmat = const.tile([P, B], BF16, name="lmat")
         rmat = const.tile([P, OUT], BF16, name="rmat")
         nc.vector.memset(lmat[:], 0.0)
@@ -109,15 +115,15 @@ def tile_optimizedlinear_kernel(tc, input_data, weight, bias, prev_grad, prev_bi
         nc.vector.tensor_copy(out=rmat[0:1, :], in_=stage[0:1, 0:OUT])
         nc.vector.tensor_copy(out=rmat[32:33, :], in_=stage[32:33, 0:OUT])
         nc.vector.tensor_copy(out=lrc[:], in_=lrb[:])
-        dsb = const.tile([P, NC, NB, CW], F32, name="dsb")
+        dsb = const.tile([P, NM, CW], F32, name="dsb")
 
-        def deint(u, t):
+        def deint(u):
             if u >= NU or u < DEI_FROM:
                 return
-            d = deip.tile([P, PASSES, 2, P], F32, name="dei")
-            dei[2 * u + t] = d
-            src = raw[2 * u + t][:].bitcast(F32).rearrange("p (g j w) -> p g w j", g=PASSES, w=2)
-            if DEI_PATTERN[t] == "v":
+            d = deip.tile([P, 2 * PASSES, 2, P], F32, name="dei")
+            dei[u] = d
+            src = raw[u][:].rearrange("p t k -> p (t k)").bitcast(F32).rearrange("p (a j w) -> p a w j", a=2 * PASSES, w=2)
+            if DEI_ENG == "v":
                 nc.vector.tensor_copy(out=d[:], in_=src)
             else:
                 nc.scalar.copy(out=d[:], in_=src)
@@ -132,10 +138,10 @@ def tile_optimizedlinear_kernel(tc, input_data, weight, bias, prev_grad, prev_bi
                     for g2 in range(2):
                         g = 2 * half + g2
                         for w in range(2):
-                            if 2 * u + t in dei:
-                                src = dei[2 * u + t][:, g, w, :]
+                            if u in dei:
+                                src = dei[u][:, t * PASSES + g, w, :]
                             else:
-                                src = raw[2 * u + t][:].bitcast(F32)[:, 256 * g + w:256 * (g + 1):2]
+                                src = raw[u][:, t, :].bitcast(F32)[:, 256 * g + w:256 * (g + 1):2]
                             nc.tensor.transpose(bank[:, 2 * g2 + w, :], src, ident[:])
                     dst = gview[:, 2 * half:2 * half + 2, t * P:(t + 1) * P, :]
                     srcb = bank[:].rearrange("p (g w) r -> p g r w", w=2)
@@ -143,99 +149,90 @@ def tile_optimizedlinear_kernel(tc, input_data, weight, bias, prev_grad, prev_bi
                         nc.scalar.copy(out=dst, in_=srcb)
                     else:
                         nc.vector.tensor_copy(out=dst, in_=srcb)
-            state["freed"] = 2 * u + 2
+            state["freed"] = u + 1
 
         def quant(u):
             kind, idx = units[u][0], units[u][1]
             nbufs = 2 if kind == "x" else COD_BUFS
-            cc = codp.tile([P, PASSES * CW], U32, name=kind + "cod", bufs=nbufs, align_bytes=64)
-            ss = codp.tile([P, PASSES * CW], U8, name=kind + "scl", bufs=nbufs, align_bytes=64)
+            cc = codp.tile([P, PASSES * UR], U32, name=kind + "cod", bufs=nbufs, align_bytes=64)
+            ss = codp.tile([P, PASSES * UR], U8, name=kind + "scl", bufs=nbufs, align_bytes=64)
             cod[(kind, idx)] = (cc, ss)
             nc.vector.quantize_mx(out=cc[:].bitcast(FP8X4), scales=ss[:], in_=grp[u][:])
 
-        def dmm(n, eng):
-            if n >= NC * NB // 2:
+        def dmm(n):
+            if n >= NM:
                 return
-            c, i = n // 2, 2 * (n % 2)
-            cols = slice(c * CW, (c + 1) * CW)
-            dps = tpp.tile([P, 2, CW], F32, name="bank")
-            for q in range(2):
-                nc.tensor.matmul(out=dps[:, q, :], lhsT=lmat[:, (i + q) * P:(i + q + 1) * P], rhs=rmat[:, cols], start=True, stop=True)
-            if eng == "s":
-                nc.scalar.copy(out=dsb[:, c, i:i + 2, :], in_=dps[:])
+            c, i = n // NB, n % NB
+            dps = tpp.tile([P, CW], F32, name="bank")
+            nc.tensor.matmul(out=dps[:], lhsT=lmat[:, i * P:(i + 1) * P], rhs=rmat[:, c * CW:(c + 1) * CW], start=True, stop=True)
+            if (DEV_HEAD if n < DEI_FROM else DEV) == "s":
+                nc.scalar.copy(out=dsb[:, n, :], in_=dps[:])
             else:
-                nc.vector.tensor_copy(out=dsb[:, c, i:i + 2, :], in_=dps[:])
+                nc.vector.tensor_copy(out=dsb[:, n, :], in_=dps[:])
 
         def mrun(j):
-            c, h = j // 2, j % 2
-            xc, xs = cod[("x", h)]
-            last = j == NM - 1
-            for t in range(2):
-                if last:
-                    pbk = tpp.tile([P, CW], F32, name="bank")
-                    bbk = accp.tile([P, CW], F32, name="acc")
-                    acc[(j, t)] = [bbk[:], pbk[:]]
-                else:
-                    bk = accp.tile([P, 2, CW], F32, name="acc")
-                    acc[(j, t)] = [bk[:, 0, :], bk[:, 1, :]]
-            order = [(1, 0), (1, 1), (0, 0), (0, 1)] if last else [(1, 0), (0, 0), (1, 1), (0, 1)]
-            for (m, t) in order:
-                cc, ss = cod[("wg"[m], c)]
-                for g in range(PASSES):
-                    xsl = slice(g * CW + t * P, g * CW + (t + 1) * P)
-                    ws = slice(g * CW, (g + 1) * CW)
-                    nc.tensor.matmul_mx(out=acc[(j, t)][m], lhsT=xc[:, xsl].bitcast(FP8X4), lhsT_scale=xs[:, xsl],
-                                        rhs=cc[:, ws].bitcast(FP8X4), rhs_scale=ss[:, ws],
-                                        start=(g == 0), stop=(g == PASSES - 1))
+            c, i = j // NB, j % NB
+            xc, xs = cod[("x", i // 2)]
+            pbk = accp.tile([P, 2, UR], F32, name="acc")
+            bbk = accp.tile([P, 2, UR], F32, name="acc")
+            acc[j] = (bbk, pbk)
+            for m in (1, 0):
+                for h in range(2):
+                    cc, ss = cod[("wg"[m], 2 * c + h)]
+                    for g in range(PASSES):
+                        xsl = slice(g * UR + (i % 2) * P, g * UR + (i % 2 + 1) * P)
+                        ws = slice(g * UR, (g + 1) * UR)
+                        nc.tensor.matmul_mx(out=acc[j][m][:, h, :], lhsT=xc[:, xsl].bitcast(FP8X4), lhsT_scale=xs[:, xsl],
+                                            rhs=cc[:, ws].bitcast(FP8X4), rhs_scale=ss[:, ws],
+                                            start=(g == 0), stop=(g == PASSES - 1))
 
         def epi_a(j):
-            c, h = j // 2, j % 2
-            for t in range(2):
-                i = 2 * h + t
-                tt = epp.tile([P, CW], F32, name="t")
-                tmp[(j, t)] = tt
-                nc.vector.scalar_tensor_tensor(out=tt[:], in0=acc[(j, t)][1], scalar=lrc[:, i:i + 1],
-                                               in1=dsb[:, c, i, :], op0=ALU.mult, op1=ALU.add)
+            i = j % NB
+            tt = epp.tile([P, CW], F32, name="t")
+            tmp[j] = tt
+            nc.vector.scalar_tensor_tensor(out=tt[:], in0=acc[j][1][:].rearrange("p h o -> p (h o)"), scalar=lrc[:, i:i + 1],
+                                           in1=dsb[:, j, :], op0=ALU.mult, op1=ALU.add)
 
         def epi_b(j):
-            c, h = j // 2, j % 2
+            c, i = j // NB, j % NB
             cols = slice(c * CW, (c + 1) * CW)
-            for t in range(2):
-                i = 2 * h + t
-                rws = slice(i * P, (i + 1) * P)
-                o = epp.tile([P, CW], F32, name="o", bufs=8)
-                nc.vector.tensor_tensor(out=o[:], in0=acc[(j, t)][0], in1=tmp[(j, t)][:], op=ALU.subtract)
-                f8 = epp.tile([P, CW], FP8, name="f8", bufs=12)
-                if CAST_ON == "s":
-                    nc.scalar.activation(out=f8[:], in_=o[:], func=ACT.Copy, scale=Y_SCALE, saturate=False)
-                else:
-                    nc.vector.tensor_scalar(out=f8[:], in0=o[:], scalar1=Y_SCALE, scalar2=None, op0=ALU.mult, saturate=False)
-                if STORE_ON == "s":
-                    nc.scalar.dma_start(out=out_0[rws, cols], in_=o[:])
-                else:
-                    nc.sync.dma_start(out=out_0[rws, cols], in_=o[:])
-                nc.sync.dma_start(out=out_1[rws, cols], in_=f8[:].bitcast(U8))
+            rws = slice(i * P, (i + 1) * P)
+            o = epp.tile([P, CW], F32, name="o", bufs=5)
+            nc.vector.tensor_tensor(out=o[:], in0=acc[j][0][:].rearrange("p h o -> p (h o)"), in1=tmp[j][:], op=ALU.subtract)
+            f8 = epp.tile([P, CW], FP8, name="f8", bufs=6)
+            nc.scalar.activation(out=f8[:], in_=o[:], func=ACT.Copy, scale=Y_SCALE, saturate=False)
+            if STORE_ON == "s":
+                nc.scalar.dma_start(out=out_0[rws, cols], in_=o[:])
+            else:
+                nc.sync.dma_start(out=out_0[rws, cols], in_=o[:])
+            nc.sync.dma_start(out=out_1[rws, cols], in_=f8[:].bitcast(U8))
 
-        deint(0, 0)
-        deint(0, 1)
-        for s in range(NM + LEAD - 1):
-            j = s - LEAD + 1 if s >= LEAD else (0 if s == 3 else -1)
-            if s == LEAD - 1 and LEAD > 4:
-                j = -1
-            if s < NU:
-                trun(s)
-                dmm(s, DEV[s % 2])
+        for u in range(DEI_AHEAD):
+            deint(u)
+        pend_q = -1
+        pend_e = -1
+        for (what, n) in seq:
+            if what == "T":
+                trun(n)
                 load()
-                load()
-            if 1 <= s <= NU:
-                quant(s - 1)
-            if j >= 0:
-                mrun(j)
-            if j >= 1:
-                epi_a(j - 1)
-            deint(s + 1, 0)
-            if j >= 1:
-                epi_b(j - 1)
-            deint(s + 1, 1)
-        epi_a(NM - 1)
-        epi_b(NM - 1)
+                if pend_q >= 0:
+                    quant(pend_q)
+                pend_q = n
+                dmm(n)
+                if pend_e >= 0:
+                    epi_a(pend_e)
+                deint(n + DEI_AHEAD)
+                if pend_e >= 0:
+                    epi_b(pend_e)
+                pend_e = -1
+            else:
+                if pend_q >= 0:
+                    quant(pend_q)
+                pend_q = -1
+                mrun(n)
+                if pend_e >= 0:
+                    epi_a(pend_e)
+                    epi_b(pend_e)
+                pend_e = n
+        epi_a(pend_e)
+        epi_b(pend_e)

@@ -18,221 +18,201 @@ ACT = mybir.ActivationFunctionType
 
 P = 128
 PASSES = IN // 512
-NB = B // P
-UR = 256
-CW = 512
-NC = OUT // CW
+X_TILES = B // P
+CHUNK = 256
+N_CHUNKS = OUT // CHUNK
+N_UNITS = 2 + 2 * N_CHUNKS
+N_MRUNS = 2 * N_CHUNKS
+N_STEPS = N_MRUNS + 4
 
-DEI_FROM = 6
-DEI_ENG = "v"
-CO = "ssss"
-DEV_HEAD = "v"
-DEV = "s"
-RAW_BUFS = 6
-DEI_BUFS = 3
-COD_BUFS = 4
-STORE_ON = "s"
-EXTRA_T_BEFORE = 3
-DEI_AHEAD = 1
+FIRST_SORTED_UNIT = 4
+
+RAW_TILES = 12
+SORTED_TILES = 6
+GROUPED_TILES = 3
+CODE_TILES = 4
+T_TILES = 4
+RESULT_TILES = 8
+BYTE_TILES = 12
 
 
 def tile_optimizedlinear_kernel(tc, input_data, weight, bias, prev_grad, prev_bias_grad, lr_samples, out_0, out_1):
     nc = tc.nc
 
-    units = [("x", 0, input_data, 0)]
-    for c in range(NC):
-        for h in range(2):
-            units.append(("w", 2 * c + h, weight, c * CW + h * UR))
-            units.append(("g", 2 * c + h, prev_grad, c * CW + h * UR))
-        if c == 0:
-            units.append(("x", 1, input_data, UR))
-    NU = len(units)
-    NM = NC * NB
-
-    seq = [("T", u) for u in range(6)]
-    nxt = 6
-    for j in range(NM):
-        if j == EXTRA_T_BEFORE and nxt < NU:
-            seq.append(("T", nxt))
-            nxt += 1
-        seq.append(("M", j))
-        if nxt < NU:
-            seq.append(("T", nxt))
-            nxt += 1
+    units = [("x", 0, input_data, 0), ("w", 0, weight, 0), ("g", 0, prev_grad, 0), ("x", 1, input_data, CHUNK)]
+    for c in range(1, N_CHUNKS):
+        units.append(("w", c, weight, c * CHUNK))
+        units.append(("g", c, prev_grad, c * CHUNK))
 
     with ExitStack() as ctx:
         const = ctx.enter_context(tc.tile_pool(name="const", bufs=1))
-        rawp = ctx.enter_context(tc.tile_pool(name="rawp", bufs=RAW_BUFS))
-        deip = ctx.enter_context(tc.tile_pool(name="deip", bufs=DEI_BUFS))
-        grpp = ctx.enter_context(tc.tile_pool(name="grpp", bufs=3))
-        codp = ctx.enter_context(tc.tile_pool(name="codp", bufs=COD_BUFS))
-        epp = ctx.enter_context(tc.tile_pool(name="epp", bufs=3))
-        tpp = ctx.enter_context(tc.psum_pool(name="tpp", bufs=4))
-        accp = ctx.enter_context(tc.psum_pool(name="accp", bufs=4))
+        raw_pool = ctx.enter_context(tc.tile_pool(name="raw", bufs=RAW_TILES))
+        sorted_pool = ctx.enter_context(tc.tile_pool(name="sorted", bufs=SORTED_TILES))
+        grouped_pool = ctx.enter_context(tc.tile_pool(name="grouped", bufs=GROUPED_TILES))
+        code_pool = ctx.enter_context(tc.tile_pool(name="codes", bufs=CODE_TILES))
+        result_pool = ctx.enter_context(tc.tile_pool(name="result", bufs=T_TILES))
+        turn_psum = ctx.enter_context(tc.psum_pool(name="turn", bufs=4))
+        acc_psum = ctx.enter_context(tc.psum_pool(name="acc", bufs=4))
         ctx.enter_context(tc.manual_schedule())
 
         raw = {}
-        dei = {}
-        grp = {}
-        cod = {}
+        by_parity = {}
+        grouped = {}
+        codes = {}
         acc = {}
-        tmp = {}
-        state = {"loaded": 0, "freed": 0}
+        t_tiles = {}
+        progress = {"loaded": 0, "transposed": 0}
 
-        def load():
-            u = state["loaded"]
-            if u >= NU or u - state["freed"] >= RAW_BUFS:
+        def load_row_tile():
+            n = progress["loaded"]
+            if n >= 2 * N_UNITS or n - progress["transposed"] >= RAW_TILES:
                 return
-            state["loaded"] += 1
-            kind, idx, src, r0 = units[u]
-            tl = rawp.tile([P, 2, IN], BF16, name="raw")
-            raw[u] = tl
-            for t in range(2):
-                nc.sync.dma_start(out=tl[:, t, :], in_=src[r0 + t * P:r0 + (t + 1) * P, :])
+            progress["loaded"] += 1
+            kind, index, src, first_row = units[n // 2]
+            rows = slice(first_row + (n % 2) * P, first_row + (n % 2 + 1) * P)
+            tile = raw_pool.tile([P, IN], BF16, name="raw")
+            raw[n] = tile
+            pieces = 2 if n == 0 else 1
+            for q in range(pieces):
+                cols = slice(q * IN // pieces, (q + 1) * IN // pieces)
+                nc.sync.dma_start(out=tile[:, cols], in_=src[rows, cols])
 
-        stage = const.tile([P, OUT + B], BF16, name="stage")
-        lrb = const.tile([P, NB], BF16, name="lrb")
-        nc.scalar.dma_start(out=stage[0:1, 0:OUT], in_=prev_bias_grad.rearrange("(a b) -> a b", a=1))
-        nc.scalar.dma_start(out=stage[32:33, 0:OUT], in_=bias.rearrange("(a b) -> a b", a=1))
-        nc.scalar.dma_start(out=stage[0:1, OUT:OUT + B], in_=lr_samples.rearrange("(a b) -> a b", a=1))
-        with nc.allow_non_contiguous_dma(reason="lr, one value to a partition"):
-            nc.scalar.dma_start(out=lrb[:], in_=lr_samples.rearrange("(i p) -> p i", p=P))
-        for n in range(RAW_BUFS):
-            load()
-        lmat = const.tile([P, B], BF16, name="lmat")
-        rmat = const.tile([P, OUT], BF16, name="rmat")
-        nc.vector.memset(lmat[:], 0.0)
-        nc.vector.memset(lmat[32:64, :], -1.0)
-        nc.vector.memset(rmat[:], 0.0)
-        ident = const.tile([P, P], F32, name="ident")
-        make_identity(nc, ident[:])
-        lrc = const.tile([P, NB], F32, name="lrc")
-        warm = const.tile([P, 1], F32, name="warm")
-        nc.vector.memset(warm[:], 0.0)
-        warm2 = const.tile([P, 1], F32, name="warm2")
-        nc.scalar.activation(out=warm2[:], in_=warm[:], func=ACT.Copy, scale=1.0)
-        nc.vector.tensor_copy(out=lmat[0:1, :], in_=stage[0:1, OUT:OUT + B])
-        nc.vector.tensor_copy(out=rmat[0:1, :], in_=stage[0:1, 0:OUT])
-        nc.vector.tensor_copy(out=rmat[32:33, :], in_=stage[32:33, 0:OUT])
-        nc.vector.tensor_copy(out=lrc[:], in_=lrb[:])
-        dsb = const.tile([P, NM, CW], F32, name="dsb")
+        rows_in = const.tile([P, OUT + B], BF16, name="rows_in")
+        lr_bf16 = const.tile([P, X_TILES], BF16, name="lr_bf16")
+        nc.scalar.dma_start(out=rows_in[0:1, 0:OUT], in_=prev_bias_grad.rearrange("(a b) -> a b", a=1))
+        nc.scalar.dma_start(out=rows_in[32:33, 0:OUT], in_=bias.rearrange("(a b) -> a b", a=1))
+        nc.scalar.dma_start(out=rows_in[0:1, OUT:OUT + B], in_=lr_samples.rearrange("(a b) -> a b", a=1))
+        with nc.allow_non_contiguous_dma(reason="lr_samples, one value to a partition: 512 elements in all"):
+            nc.scalar.dma_start(out=lr_bf16[:], in_=lr_samples.rearrange("(i p) -> p i", p=P))
+        for n in range(RAW_TILES):
+            load_row_tile()
 
-        def deint(u):
-            if u >= NU or u < DEI_FROM:
+        d_lhsT = const.tile([P, B], BF16, name="d_lhsT")
+        d_rhs = const.tile([P, OUT], BF16, name="d_rhs")
+        nc.vector.memset(d_lhsT[:], 0.0)
+        nc.vector.memset(d_lhsT[32:64, :], -1.0)
+        nc.vector.memset(d_rhs[:], 0.0)
+        identity = const.tile([P, P], F32, name="identity")
+        make_identity(nc, identity[:])
+        lr = const.tile([P, X_TILES], F32, name="lr")
+        dummy_in = const.tile([P, 1], F32, name="dummy_in")
+        nc.vector.memset(dummy_in[:], 0.0)
+        dummy_out = const.tile([P, 1], F32, name="dummy_out")
+        nc.scalar.activation(out=dummy_out[:], in_=dummy_in[:], func=ACT.Copy, scale=1.0)
+        nc.vector.tensor_copy(out=d_lhsT[0:1, :], in_=rows_in[0:1, OUT:OUT + B])
+        nc.vector.tensor_copy(out=d_rhs[0:1, :], in_=rows_in[0:1, 0:OUT])
+        nc.vector.tensor_copy(out=d_rhs[32:33, :], in_=rows_in[32:33, 0:OUT])
+        nc.vector.tensor_copy(out=lr[:], in_=lr_bf16[:])
+        d_sbuf = const.tile([P, N_CHUNKS, X_TILES, CHUNK], F32, name="d_sbuf")
+
+        def sort_words(u, t):
+            if u >= N_UNITS or u < FIRST_SORTED_UNIT:
                 return
-            d = deip.tile([P, 2 * PASSES, 2, P], F32, name="dei")
-            dei[u] = d
-            src = raw[u][:].rearrange("p t k -> p (t k)").bitcast(F32).rearrange("p (a j w) -> p a w j", a=2 * PASSES, w=2)
-            if DEI_ENG == "v":
-                nc.vector.tensor_copy(out=d[:], in_=src)
-            else:
-                nc.scalar.copy(out=d[:], in_=src)
+            tile = sorted_pool.tile([P, PASSES, 2, P], F32, name="by_parity")
+            by_parity[2 * u + t] = tile
+            nc.vector.tensor_copy(out=tile[:], in_=raw[2 * u + t][:].bitcast(F32).rearrange("p (g j v) -> p g v j", g=PASSES, v=2))
 
-        def trun(u):
-            g_tile = grpp.tile([P, 4096], BF16, name="grp", align_bytes=64)
-            grp[u] = g_tile
-            gview = g_tile[:].bitcast(F32).rearrange("p (g o w) -> p g o w", g=PASSES, w=2)
+        def transpose_unit(u):
+            tile = grouped_pool.tile([P, PASSES * CHUNK * 4], BF16, name="grouped", align_bytes=64)
+            grouped[u] = tile
+            words = tile[:].bitcast(F32).rearrange("p (g r v) -> p g r v", g=PASSES, v=2)
             for t in range(2):
                 for half in range(2):
-                    bank = tpp.tile([P, 4, P], F32, name="bank")
+                    bank = turn_psum.tile([P, 4, P], F32, name="bank")
                     for g2 in range(2):
                         g = 2 * half + g2
-                        for w in range(2):
-                            if u in dei:
-                                src = dei[u][:, t * PASSES + g, w, :]
+                        for v in range(2):
+                            if 2 * u + t in by_parity:
+                                src = by_parity[2 * u + t][:, g, v, :]
                             else:
-                                src = raw[u][:, t, :].bitcast(F32)[:, 256 * g + w:256 * (g + 1):2]
-                            nc.tensor.transpose(bank[:, 2 * g2 + w, :], src, ident[:])
-                    dst = gview[:, 2 * half:2 * half + 2, t * P:(t + 1) * P, :]
-                    srcb = bank[:].rearrange("p (g w) r -> p g r w", w=2)
-                    if CO[2 * t + half] == "s":
-                        nc.scalar.copy(out=dst, in_=srcb)
-                    else:
-                        nc.vector.tensor_copy(out=dst, in_=srcb)
-            state["freed"] = u + 1
+                                src = raw[2 * u + t][:].bitcast(F32)[:, 256 * g + v:256 * (g + 1):2]
+                            nc.tensor.transpose(bank[:, 2 * g2 + v, :], src, identity[:])
+                    nc.scalar.copy(out=words[:, 2 * half:2 * half + 2, t * P:(t + 1) * P, :],
+                                   in_=bank[:].rearrange("p (g v) r -> p g r v", v=2))
+            progress["transposed"] = 2 * u + 2
 
-        def quant(u):
-            kind, idx = units[u][0], units[u][1]
-            nbufs = 2 if kind == "x" else COD_BUFS
-            cc = codp.tile([P, PASSES * UR], U32, name=kind + "cod", bufs=nbufs, align_bytes=64)
-            ss = codp.tile([P, PASSES * UR], U8, name=kind + "scl", bufs=nbufs, align_bytes=64)
-            cod[(kind, idx)] = (cc, ss)
-            nc.vector.quantize_mx(out=cc[:].bitcast(FP8X4), scales=ss[:], in_=grp[u][:])
+        def quantize_unit(u):
+            kind, index = units[u][0], units[u][1]
+            bufs = 2 if kind == "x" else CODE_TILES
+            cod = code_pool.tile([P, PASSES * CHUNK], U32, name=kind + "_codes", bufs=bufs, align_bytes=64)
+            scl = code_pool.tile([P, PASSES * CHUNK], U8, name=kind + "_scales", bufs=bufs, align_bytes=64)
+            codes[(kind, index)] = (cod, scl)
+            nc.vector.quantize_mx(out=cod[:].bitcast(FP8X4), scales=scl[:], in_=grouped[u][:])
 
-        def dmm(n):
-            if n >= NM:
+        def bias_term(n):
+            if n >= N_MRUNS:
                 return
-            c, i = n // NB, n % NB
-            dps = tpp.tile([P, CW], F32, name="bank")
-            nc.tensor.matmul(out=dps[:], lhsT=lmat[:, i * P:(i + 1) * P], rhs=rmat[:, c * CW:(c + 1) * CW], start=True, stop=True)
-            if (DEV_HEAD if n < DEI_FROM else DEV) == "s":
-                nc.scalar.copy(out=dsb[:, n, :], in_=dps[:])
-            else:
-                nc.vector.tensor_copy(out=dsb[:, n, :], in_=dps[:])
+            c, i = n // 2, 2 * (n % 2)
+            bank = turn_psum.tile([P, 2, CHUNK], F32, name="bank")
+            for q in range(2):
+                nc.tensor.matmul(out=bank[:, q, :], lhsT=d_lhsT[:, (i + q) * P:(i + q + 1) * P],
+                                 rhs=d_rhs[:, c * CHUNK:(c + 1) * CHUNK], start=True, stop=True)
+            nc.scalar.copy(out=d_sbuf[:, c, i:i + 2, :], in_=bank[:])
 
-        def mrun(j):
-            c, i = j // NB, j % NB
-            xc, xs = cod[("x", i // 2)]
-            pbk = accp.tile([P, 2, UR], F32, name="acc")
-            bbk = accp.tile([P, 2, UR], F32, name="acc")
-            acc[j] = (bbk, pbk)
-            for m in (1, 0):
-                for h in range(2):
-                    cc, ss = cod[("wg"[m], 2 * c + h)]
-                    for g in range(PASSES):
-                        xsl = slice(g * UR + (i % 2) * P, g * UR + (i % 2 + 1) * P)
-                        ws = slice(g * UR, (g + 1) * UR)
-                        nc.tensor.matmul_mx(out=acc[j][m][:, h, :], lhsT=xc[:, xsl].bitcast(FP8X4), lhsT_scale=xs[:, xsl],
-                                            rhs=cc[:, ws].bitcast(FP8X4), rhs_scale=ss[:, ws],
-                                            start=(g == 0), stop=(g == PASSES - 1))
+        def multiply(j):
+            c, h = j // 2, j % 2
+            x_cod, x_scl = codes[("x", h)]
+            last = j == N_MRUNS - 1
+            for t in range(2):
+                if last:
+                    pert_bank = turn_psum.tile([P, CHUNK], F32, name="bank")
+                    base_bank = acc_psum.tile([P, CHUNK], F32, name="acc")
+                    acc[(j, t)] = [base_bank[:], pert_bank[:]]
+                else:
+                    bank = acc_psum.tile([P, 2, CHUNK], F32, name="acc")
+                    acc[(j, t)] = [bank[:, 0, :], bank[:, 1, :]]
+            order = [(1, 0), (1, 1), (0, 0), (0, 1)] if last else [(1, 0), (0, 0), (1, 1), (0, 1)]
+            for (m, t) in order:
+                w_cod, w_scl = codes[("wg"[m], c)]
+                for g in range(PASSES):
+                    x_cols = slice(g * CHUNK + t * P, g * CHUNK + (t + 1) * P)
+                    w_cols = slice(g * CHUNK, (g + 1) * CHUNK)
+                    nc.tensor.matmul_mx(out=acc[(j, t)][m], lhsT=x_cod[:, x_cols].bitcast(FP8X4), lhsT_scale=x_scl[:, x_cols],
+                                        rhs=w_cod[:, w_cols].bitcast(FP8X4), rhs_scale=w_scl[:, w_cols],
+                                        start=(g == 0), stop=(g == PASSES - 1))
 
-        def epi_a(j):
-            i = j % NB
-            tt = epp.tile([P, CW], F32, name="t")
-            tmp[j] = tt
-            nc.vector.scalar_tensor_tensor(out=tt[:], in0=acc[j][1][:].rearrange("p h o -> p (h o)"), scalar=lrc[:, i:i + 1],
-                                           in1=dsb[:, j, :], op0=ALU.mult, op1=ALU.add)
+        def scale_pert(j):
+            c, h = j // 2, j % 2
+            for t in range(2):
+                i = 2 * h + t
+                tile = result_pool.tile([P, CHUNK], F32, name="t")
+                t_tiles[(j, t)] = tile
+                nc.vector.scalar_tensor_tensor(out=tile[:], in0=acc[(j, t)][1], scalar=lr[:, i:i + 1],
+                                               in1=d_sbuf[:, c, i, :], op0=ALU.mult, op1=ALU.add)
 
-        def epi_b(j):
-            c, i = j // NB, j % NB
-            cols = slice(c * CW, (c + 1) * CW)
-            rws = slice(i * P, (i + 1) * P)
-            o = epp.tile([P, CW], F32, name="o", bufs=5)
-            nc.vector.tensor_tensor(out=o[:], in0=acc[j][0][:].rearrange("p h o -> p (h o)"), in1=tmp[j][:], op=ALU.subtract)
-            f8 = epp.tile([P, CW], FP8, name="f8", bufs=6)
-            nc.scalar.activation(out=f8[:], in_=o[:], func=ACT.Copy, scale=Y_SCALE, saturate=False)
-            if STORE_ON == "s":
-                nc.scalar.dma_start(out=out_0[rws, cols], in_=o[:])
-            else:
-                nc.sync.dma_start(out=out_0[rws, cols], in_=o[:])
-            nc.sync.dma_start(out=out_1[rws, cols], in_=f8[:].bitcast(U8))
+        def finish(j):
+            c, h = j // 2, j % 2
+            cols = slice(c * CHUNK, (c + 1) * CHUNK)
+            for t in range(2):
+                rows = slice((2 * h + t) * P, (2 * h + t + 1) * P)
+                result = result_pool.tile([P, CHUNK], F32, name="result", bufs=RESULT_TILES)
+                nc.vector.tensor_tensor(out=result[:], in0=acc[(j, t)][0], in1=t_tiles[(j, t)][:], op=ALU.subtract)
+                as_fp8 = result_pool.tile([P, CHUNK], FP8, name="as_fp8", bufs=BYTE_TILES)
+                nc.scalar.activation(out=as_fp8[:], in_=result[:], func=ACT.Copy, scale=Y_SCALE, saturate=False)
+                nc.sync.dma_start(out=out_0[rows, cols], in_=result[:])
+                nc.sync.dma_start(out=out_1[rows, cols], in_=as_fp8[:].bitcast(U8))
 
-        for u in range(DEI_AHEAD):
-            deint(u)
-        pend_q = -1
-        pend_e = -1
-        for (what, n) in seq:
-            if what == "T":
-                trun(n)
-                load()
-                if pend_q >= 0:
-                    quant(pend_q)
-                pend_q = n
-                dmm(n)
-                if pend_e >= 0:
-                    epi_a(pend_e)
-                deint(n + DEI_AHEAD)
-                if pend_e >= 0:
-                    epi_b(pend_e)
-                pend_e = -1
-            else:
-                if pend_q >= 0:
-                    quant(pend_q)
-                pend_q = -1
-                mrun(n)
-                if pend_e >= 0:
-                    epi_a(pend_e)
-                    epi_b(pend_e)
-                pend_e = n
-        epi_a(pend_e)
-        epi_b(pend_e)
+        def mrun_of_step(s):
+            if s == 3:
+                return 0
+            return s - 4 if s >= 5 else -1
+
+        for s in range(N_STEPS):
+            j = mrun_of_step(s)
+            if s < N_UNITS:
+                transpose_unit(s)
+                bias_term(s)
+                load_row_tile()
+                load_row_tile()
+            if 1 <= s <= N_UNITS:
+                quantize_unit(s - 1)
+            if j >= 0:
+                multiply(j)
+            if j >= 1:
+                scale_pert(j - 1)
+            sort_words(s + 1, 0)
+            if j >= 1:
+                finish(j - 1)
+            sort_words(s + 1, 1)
+        scale_pert(N_MRUNS - 1)
+        finish(N_MRUNS - 1)

@@ -25,7 +25,7 @@ N_UNITS = 2 + 2 * N_CHUNKS
 N_MRUNS = 2 * N_CHUNKS
 N_STEPS = N_MRUNS + 4
 
-FIRST_SORTED_UNIT = 4
+FIRST_SORTED_UNIT = 1
 
 RAW_TILES = 12
 SORTED_TILES = 6

@@ -24,25 +24,29 @@ N_CHUNKS = OUT // CHUNK
 N_UNITS = 2 + 2 * N_CHUNKS
 N_MRUNS = 2 * N_CHUNKS
 N_STEPS = N_MRUNS + 4
+D_COLS = 512
+N_D = X_TILES * OUT // D_COLS
 
 FIRST_SORTED_UNIT = 1
+SCALAR_SORT_EVERY = 2
+FIRST_SCALAR_SORT = 11
 
 RAW_TILES = 12
 SORTED_TILES = 6
 GROUPED_TILES = 3
 CODE_TILES = 4
-T_TILES = 4
-RESULT_TILES = 8
-BYTE_TILES = 12
+T_TILES = 2
+RESULT_TILES = 4
+BYTE_TILES = 6
 
 
 def tile_optimizedlinear_kernel(tc, input_data, weight, bias, prev_grad, prev_bias_grad, lr_samples, out_0, out_1):
     nc = tc.nc
 
-    units = [("x", 0, input_data, 0), ("w", 0, weight, 0), ("g", 0, prev_grad, 0), ("x", 1, input_data, CHUNK)]
+    units = [("x", 0, input_data, 0), ("g", 0, prev_grad, 0), ("w", 0, weight, 0), ("x", 1, input_data, CHUNK)]
     for c in range(1, N_CHUNKS):
-        units.append(("w", c, weight, c * CHUNK))
         units.append(("g", c, prev_grad, c * CHUNK))
+        units.append(("w", c, weight, c * CHUNK))
 
     with ExitStack() as ctx:
         const = ctx.enter_context(tc.tile_pool(name="const", bufs=1))
@@ -60,7 +64,9 @@ def tile_optimizedlinear_kernel(tc, input_data, weight, bias, prev_grad, prev_bi
         grouped = {}
         codes = {}
         acc = {}
+        whole = {}
         t_tiles = {}
+        spread_banks = {}
         progress = {"loaded": 0, "transposed": 0}
 
         def load_row_tile():
@@ -77,21 +83,21 @@ def tile_optimizedlinear_kernel(tc, input_data, weight, bias, prev_grad, prev_bi
                 cols = slice(q * IN // pieces, (q + 1) * IN // pieces)
                 nc.sync.dma_start(out=tile[:, cols], in_=src[rows, cols])
 
-        rows_in = const.tile([P, OUT + B], BF16, name="rows_in")
+        rows_in = const.tile([P, OUT], BF16, name="rows_in")
         lr_bf16 = const.tile([P, X_TILES], BF16, name="lr_bf16")
-        nc.scalar.dma_start(out=rows_in[0:1, 0:OUT], in_=prev_bias_grad.rearrange("(a b) -> a b", a=1))
-        nc.scalar.dma_start(out=rows_in[32:33, 0:OUT], in_=bias.rearrange("(a b) -> a b", a=1))
-        nc.scalar.dma_start(out=rows_in[0:1, OUT:OUT + B], in_=lr_samples.rearrange("(a b) -> a b", a=1))
+        nc.scalar.dma_start(out=rows_in[0:1, :], in_=prev_bias_grad.rearrange("(a b) -> a b", a=1))
+        nc.scalar.dma_start(out=rows_in[32:33, :], in_=bias.rearrange("(a b) -> a b", a=1))
         with nc.allow_non_contiguous_dma(reason="lr_samples, one value to a partition: 512 elements in all"):
             nc.scalar.dma_start(out=lr_bf16[:], in_=lr_samples.rearrange("(i p) -> p i", p=P))
         for n in range(RAW_TILES):
             load_row_tile()
 
-        d_lhsT = const.tile([P, B], BF16, name="d_lhsT")
-        d_rhs = const.tile([P, OUT], BF16, name="d_rhs")
-        nc.vector.memset(d_lhsT[:], 0.0)
-        nc.vector.memset(d_lhsT[32:64, :], -1.0)
-        nc.vector.memset(d_rhs[:], 0.0)
+        selector = const.tile([P, 2, P], BF16, name="selector")
+        vectors = const.tile([P, OUT], BF16, name="vectors")
+        nc.vector.memset(selector[:], 0.0)
+        nc.vector.memset(selector[0:32, 0, :], 1.0)
+        nc.vector.memset(selector[32:64, 1, :], 1.0)
+        nc.vector.memset(vectors[:], 0.0)
         identity = const.tile([P, P], F32, name="identity")
         make_identity(nc, identity[:])
         lr = const.tile([P, X_TILES], F32, name="lr")
@@ -99,18 +105,26 @@ def tile_optimizedlinear_kernel(tc, input_data, weight, bias, prev_grad, prev_bi
         nc.vector.memset(dummy_in[:], 0.0)
         dummy_out = const.tile([P, 1], F32, name="dummy_out")
         nc.scalar.activation(out=dummy_out[:], in_=dummy_in[:], func=ACT.Copy, scale=1.0)
-        nc.vector.tensor_copy(out=d_lhsT[0:1, :], in_=rows_in[0:1, OUT:OUT + B])
-        nc.vector.tensor_copy(out=d_rhs[0:1, :], in_=rows_in[0:1, 0:OUT])
-        nc.vector.tensor_copy(out=d_rhs[32:33, :], in_=rows_in[32:33, 0:OUT])
+        nc.vector.tensor_copy(out=vectors[0:1, :], in_=rows_in[0:1, :])
+        nc.vector.tensor_copy(out=vectors[32:33, :], in_=rows_in[32:33, :])
         nc.vector.tensor_copy(out=lr[:], in_=lr_bf16[:])
-        d_sbuf = const.tile([P, N_CHUNKS, X_TILES, CHUNK], F32, name="d_sbuf")
+        spread = const.tile([P, 2, OUT], BF16, name="spread")
+        d_sbuf = const.tile([P, X_TILES, OUT], F32, name="d_sbuf")
 
-        def sort_words(u, t):
-            if u >= N_UNITS or u < FIRST_SORTED_UNIT:
+        def sorted_by_scalar(n):
+            return n >= FIRST_SCALAR_SORT and n % SCALAR_SORT_EVERY == FIRST_SCALAR_SORT % SCALAR_SORT_EVERY
+
+        def sort_words(n, on_scalar):
+            if n >= 2 * N_UNITS or n < 2 * FIRST_SORTED_UNIT or sorted_by_scalar(n) != on_scalar:
                 return
-            tile = sorted_pool.tile([P, PASSES, 2, P], F32, name="by_parity")
-            by_parity[2 * u + t] = tile
-            nc.vector.tensor_copy(out=tile[:], in_=raw[2 * u + t][:].bitcast(F32).rearrange("p (g j v) -> p g v j", g=PASSES, v=2))
+            view = raw[n][:].bitcast(F32).rearrange("p (g j v) -> p g v j", g=PASSES, v=2)
+            if on_scalar:
+                tile = sorted_pool.tile([P, PASSES, 2, P], F32, name="by_parity_s", bufs=2)
+                nc.scalar.copy(out=tile[:], in_=view)
+            else:
+                tile = sorted_pool.tile([P, PASSES, 2, P], F32, name="by_parity")
+                nc.vector.tensor_copy(out=tile[:], in_=view)
+            by_parity[n] = tile
 
         def transpose_unit(u):
             tile = grouped_pool.tile([P, PASSES * CHUNK * 4], BF16, name="grouped", align_bytes=64)
@@ -139,58 +153,76 @@ def tile_optimizedlinear_kernel(tc, input_data, weight, bias, prev_grad, prev_bi
             codes[(kind, index)] = (cod, scl)
             nc.vector.quantize_mx(out=cod[:].bitcast(FP8X4), scales=scl[:], in_=grouped[u][:])
 
-        def bias_term(n):
-            if n >= N_MRUNS:
+        def spread_matmuls(n):
+            if n >= 4:
                 return
-            c, i = n // 2, 2 * (n % 2)
-            bank = turn_psum.tile([P, 2, CHUNK], F32, name="bank")
+            bank = turn_psum.tile([P, OUT // 2], BF16, name="bank")
+            spread_banks[n] = bank
             for q in range(2):
-                nc.tensor.matmul(out=bank[:, q, :], lhsT=d_lhsT[:, (i + q) * P:(i + q + 1) * P],
-                                 rhs=d_rhs[:, c * CHUNK:(c + 1) * CHUNK], start=True, stop=True)
-            nc.scalar.copy(out=d_sbuf[:, c, i:i + 2, :], in_=bank[:])
+                nc.tensor.matmul(out=bank[:, q * 512:(q + 1) * 512], lhsT=selector[:, n % 2, :],
+                                 rhs=vectors[:, (n // 2) * 1024 + q * 512:(n // 2) * 1024 + (q + 1) * 512], start=True, stop=True)
+
+        def spread_copy(n):
+            if n >= 4:
+                return
+            nc.vector.tensor_copy(out=spread[:, n % 2, (n // 2) * 1024:(n // 2 + 1) * 1024], in_=spread_banks[n][:])
+
+        def bias_term(n):
+            if n < 0 or n >= N_D:
+                return
+            i, cols = n % X_TILES, slice((n // X_TILES) * D_COLS, (n // X_TILES + 1) * D_COLS)
+            nc.vector.scalar_tensor_tensor(out=d_sbuf[:, i, cols], in0=spread[:, 0, cols], scalar=lr[:, i:i + 1],
+                                           in1=spread[:, 1, cols], op0=ALU.mult, op1=ALU.subtract)
 
         def multiply(j):
             c, h = j // 2, j % 2
             x_cod, x_scl = codes[("x", h)]
             last = j == N_MRUNS - 1
-            for t in range(2):
-                if last:
-                    pert_bank = turn_psum.tile([P, CHUNK], F32, name="bank")
-                    base_bank = acc_psum.tile([P, CHUNK], F32, name="acc")
-                    acc[(j, t)] = [base_bank[:], pert_bank[:]]
+            for m in (1, 0):
+                if last and m == 0:
+                    first = turn_psum.tile([P, CHUNK], F32, name="bank")
+                    second = turn_psum.tile([P, CHUNK], F32, name="bank")
+                    acc[(j, m, 0)], acc[(j, m, 1)] = first[:], second[:]
                 else:
                     bank = acc_psum.tile([P, 2, CHUNK], F32, name="acc")
-                    acc[(j, t)] = [bank[:, 0, :], bank[:, 1, :]]
-            order = [(1, 0), (1, 1), (0, 0), (0, 1)] if last else [(1, 0), (0, 0), (1, 1), (0, 1)]
-            for (m, t) in order:
+                    acc[(j, m, 0)], acc[(j, m, 1)] = bank[:, 0, :], bank[:, 1, :]
+                    whole[(j, m)] = bank[:]
                 w_cod, w_scl = codes[("wg"[m], c)]
-                for g in range(PASSES):
-                    x_cols = slice(g * CHUNK + t * P, g * CHUNK + (t + 1) * P)
-                    w_cols = slice(g * CHUNK, (g + 1) * CHUNK)
-                    nc.tensor.matmul_mx(out=acc[(j, t)][m], lhsT=x_cod[:, x_cols].bitcast(FP8X4), lhsT_scale=x_scl[:, x_cols],
-                                        rhs=w_cod[:, w_cols].bitcast(FP8X4), rhs_scale=w_scl[:, w_cols],
-                                        start=(g == 0), stop=(g == PASSES - 1))
+                for t in range(2):
+                    for g in range(PASSES):
+                        x_cols = slice(g * CHUNK + t * P, g * CHUNK + (t + 1) * P)
+                        w_cols = slice(g * CHUNK, (g + 1) * CHUNK)
+                        nc.tensor.matmul_mx(out=acc[(j, m, t)], lhsT=x_cod[:, x_cols].bitcast(FP8X4), lhsT_scale=x_scl[:, x_cols],
+                                            rhs=w_cod[:, w_cols].bitcast(FP8X4), rhs_scale=w_scl[:, w_cols],
+                                            start=(g == 0), stop=(g == PASSES - 1))
 
         def scale_pert(j):
             c, h = j // 2, j % 2
+            tile = result_pool.tile([P, 2, CHUNK], F32, name="t")
+            t_tiles[j] = tile
             for t in range(2):
                 i = 2 * h + t
-                tile = result_pool.tile([P, CHUNK], F32, name="t")
-                t_tiles[(j, t)] = tile
-                nc.vector.scalar_tensor_tensor(out=tile[:], in0=acc[(j, t)][1], scalar=lr[:, i:i + 1],
-                                               in1=d_sbuf[:, c, i, :], op0=ALU.mult, op1=ALU.add)
+                nc.vector.scalar_tensor_tensor(out=tile[:, t, :], in0=acc[(j, 1, t)], scalar=lr[:, i:i + 1],
+                                               in1=d_sbuf[:, i, c * CHUNK:(c + 1) * CHUNK], op0=ALU.mult, op1=ALU.add)
 
         def finish(j):
             c, h = j // 2, j % 2
             cols = slice(c * CHUNK, (c + 1) * CHUNK)
-            for t in range(2):
-                rows = slice((2 * h + t) * P, (2 * h + t + 1) * P)
-                result = result_pool.tile([P, CHUNK], F32, name="result", bufs=RESULT_TILES)
-                nc.vector.tensor_tensor(out=result[:], in0=acc[(j, t)][0], in1=t_tiles[(j, t)][:], op=ALU.subtract)
-                as_fp8 = result_pool.tile([P, CHUNK], FP8, name="as_fp8", bufs=BYTE_TILES)
+            result = result_pool.tile([P, 2, CHUNK], F32, name="result", bufs=RESULT_TILES)
+            as_fp8 = result_pool.tile([P, 2, CHUNK], FP8, name="as_fp8", bufs=BYTE_TILES)
+            if (j, 0) in whole:
+                rows = slice(2 * h * P, (2 * h + 2) * P)
+                nc.vector.tensor_tensor(out=result[:], in0=whole[(j, 0)], in1=t_tiles[j][:], op=ALU.subtract)
                 nc.scalar.activation(out=as_fp8[:], in_=result[:], func=ACT.Copy, scale=Y_SCALE, saturate=False)
-                nc.sync.dma_start(out=out_0[rows, cols], in_=result[:])
-                nc.sync.dma_start(out=out_1[rows, cols], in_=as_fp8[:].bitcast(U8))
+                nc.sync.dma_start(out=out_0[rows, cols].rearrange("(t p) c -> p t c", p=P), in_=result[:])
+                nc.sync.dma_start(out=out_1[rows, cols].rearrange("(t p) c -> p t c", p=P), in_=as_fp8[:].bitcast(U8))
+            else:
+                for t in range(2):
+                    rows = slice((2 * h + t) * P, (2 * h + t + 1) * P)
+                    nc.vector.tensor_tensor(out=result[:, t, :], in0=acc[(j, 0, t)], in1=t_tiles[j][:, t, :], op=ALU.subtract)
+                    nc.scalar.activation(out=as_fp8[:, t, :], in_=result[:, t, :], func=ACT.Copy, scale=Y_SCALE, saturate=False)
+                    nc.sync.dma_start(out=out_0[rows, cols], in_=result[:, t, :])
+                    nc.sync.dma_start(out=out_1[rows, cols], in_=as_fp8[:, t, :].bitcast(U8))
 
         def mrun_of_step(s):
             if s == 3:
@@ -201,18 +233,22 @@ def tile_optimizedlinear_kernel(tc, input_data, weight, bias, prev_grad, prev_bi
             j = mrun_of_step(s)
             if s < N_UNITS:
                 transpose_unit(s)
-                bias_term(s)
+                spread_matmuls(s)
                 load_row_tile()
                 load_row_tile()
+            for n in (2 * s + 4, 2 * s + 5):
+                sort_words(n, True)
             if 1 <= s <= N_UNITS:
                 quantize_unit(s - 1)
             if j >= 0:
                 multiply(j)
             if j >= 1:
                 scale_pert(j - 1)
-            sort_words(s + 1, 0)
+            sort_words(2 * s + 2, False)
+            bias_term(s - 2)
+            spread_copy(s)
             if j >= 1:
                 finish(j - 1)
-            sort_words(s + 1, 1)
+            sort_words(2 * s + 3, False)
         scale_pert(N_MRUNS - 1)
         finish(N_MRUNS - 1)

@@ -28,7 +28,6 @@ D_COLS = 512
 N_D = X_TILES * OUT // D_COLS
 
 FIRST_SORTED_UNIT = 1
-SCALAR_SORT_EVERY = 2
 FIRST_SCALAR_SORT = 11
 
 RAW_TILES = 12
@@ -112,7 +111,7 @@ def tile_optimizedlinear_kernel(tc, input_data, weight, bias, prev_grad, prev_bi
         d_sbuf = const.tile([P, X_TILES, OUT], F32, name="d_sbuf")
 
         def sorted_by_scalar(n):
-            return n >= FIRST_SCALAR_SORT and n % SCALAR_SORT_EVERY == FIRST_SCALAR_SORT % SCALAR_SORT_EVERY
+            return n >= FIRST_SCALAR_SORT and n % 2 == 1 and (n // 2) % 3 != 0
 
         def sort_words(n, on_scalar):
             if n >= 2 * N_UNITS or n < 2 * FIRST_SORTED_UNIT or sorted_by_scalar(n) != on_scalar:

@@ -164,7 +164,7 @@ def tile_optimizedlinear_kernel(tc, input_data, weight, bias, prev_grad, prev_bi
         def spread_copy(n):
             if n >= 4:
                 return
-            nc.vector.tensor_copy(out=spread[:, n % 2, (n // 2) * 1024:(n // 2 + 1) * 1024], in_=spread_banks[n][:])
+            nc.scalar.copy(out=spread[:, n % 2, (n // 2) * 1024:(n // 2 + 1) * 1024], in_=spread_banks[n][:])
 
         def bias_term(n):
             if n < 0 or n >= N_D:
@@ -173,11 +173,11 @@ def tile_optimizedlinear_kernel(tc, input_data, weight, bias, prev_grad, prev_bi
             nc.vector.scalar_tensor_tensor(out=d_sbuf[:, i, cols], in0=spread[:, 0, cols], scalar=lr[:, i:i + 1],
                                            in1=spread[:, 1, cols], op0=ALU.mult, op1=ALU.subtract)
 
-        def multiply(j):
+        def multiply(j, halves=(1, 0)):
             c, h = j // 2, j % 2
             x_cod, x_scl = codes[("x", h)]
             last = j == N_MRUNS - 1
-            for m in (1, 0):
+            for m in halves:
                 if last and m == 0:
                     first = turn_psum.tile([P, CHUNK], F32, name="bank")
                     second = turn_psum.tile([P, CHUNK], F32, name="bank")
@@ -239,9 +239,14 @@ def tile_optimizedlinear_kernel(tc, input_data, weight, bias, prev_grad, prev_bi
                 sort_words(n, True)
             if 1 <= s <= N_UNITS:
                 quantize_unit(s - 1)
-            if j >= 0:
+            if s == 3:
+                multiply(0, (1,))
+            elif s == 4:
+                multiply(0, (0,))
+                scale_pert(0)
+            elif j >= 0:
                 multiply(j)
-            if j >= 1:
+            if j >= 2:
                 scale_pert(j - 1)
             sort_words(2 * s + 2, False)
             bias_term(s - 2)

@@ -147,8 +147,8 @@ def tile_optimizedlinear_kernel(tc, input_data, weight, bias, prev_grad, prev_bi
         def quantize_unit(u):
             kind, index = units[u][0], units[u][1]
             bufs = 2 if kind == "x" else CODE_TILES
-            cod = code_pool.tile([P, PASSES * CHUNK], U32, name=kind + "_codes", bufs=bufs, align_bytes=64)
-            scl = code_pool.tile([P, PASSES * CHUNK], U8, name=kind + "_scales", bufs=bufs, align_bytes=64)
+            cod = code_pool.tile([P, PASSES * CHUNK], U32, name=kind + "_codes", bufs=bufs, align_bytes=256)
+            scl = code_pool.tile([P, PASSES * CHUNK], U8, name=kind + "_scales", bufs=bufs, align_bytes=256)
             codes[(kind, index)] = (cod, scl)
             nc.vector.quantize_mx(out=cod[:].bitcast(FP8X4), scales=scl[:], in_=grouped[u][:])
 

@@ -28,7 +28,7 @@ D_COLS = 512
 N_D = X_TILES * OUT // D_COLS
 
 FIRST_SORTED_UNIT = 1
-FIRST_SCALAR_SORT = 11
+FIRST_SCALAR_SORT = 13
 
 RAW_TILES = 12
 SORTED_TILES = 6

@@ -24,9 +24,11 @@ N_CHUNKS = OUT // CHUNK
 N_UNITS = 2 + 2 * N_CHUNKS
 N_MRUNS = 2 * N_CHUNKS
 N_STEPS = N_MRUNS + 4
-D_COLS = 512
+D_COLS = 256
 N_D = X_TILES * OUT // D_COLS
 
+HEAD_PASSES = {2: [(0, 1)], 3: [(0, 0)], 4: [(1, 1)], 5: [(1, 0)]}
+UNSORTED_UNITS = (0, 1,)
 FIRST_SORTED_UNIT = 1
 FIRST_SCALAR_SORT = 13
 
@@ -114,7 +116,7 @@ def tile_optimizedlinear_kernel(tc, input_data, weight, bias, prev_grad, prev_bi
             return n >= FIRST_SCALAR_SORT and n % 2 == 1 and (n // 2) % 3 != 0
 
         def sort_words(n, on_scalar):
-            if n >= 2 * N_UNITS or n < 2 * FIRST_SORTED_UNIT or sorted_by_scalar(n) != on_scalar:
+            if n >= 2 * N_UNITS or n // 2 in UNSORTED_UNITS or sorted_by_scalar(n) != on_scalar:
                 return
             view = raw[n][:].bitcast(F32).rearrange("p (g j v) -> p g v j", g=PASSES, v=2)
             if on_scalar:
@@ -223,13 +225,13 @@ def tile_optimizedlinear_kernel(tc, input_data, weight, bias, prev_grad, prev_bi
                     nc.sync.dma_start(out=out_0[rows, cols], in_=result[:, t, :])
                     nc.sync.dma_start(out=out_1[rows, cols], in_=as_fp8[:, t, :].bitcast(U8))
 
-        def mrun_of_step(s):
-            if s == 3:
-                return 0
-            return s - 4 if s >= 5 else -1
+        def passes_of_step(s):
+            if s in HEAD_PASSES:
+                return HEAD_PASSES[s]
+            j = s - 4 if s >= 5 else -1
+            return [(j, 1), (j, 0)] if 0 <= j < N_MRUNS else []
 
-        for s in range(N_STEPS):
-            j = mrun_of_step(s)
+        for s in range(N_STEPS + 1):
             if s < N_UNITS:
                 transpose_unit(s)
                 spread_matmuls(s)
@@ -239,20 +241,18 @@ def tile_optimizedlinear_kernel(tc, input_data, weight, bias, prev_grad, prev_bi
                 sort_words(n, True)
             if 1 <= s <= N_UNITS:
                 quantize_unit(s - 1)
-            if s == 3:
-                multiply(0, (1,))
-            elif s == 4:
-                multiply(0, (0,))
-                scale_pert(0)
-            elif j >= 0:
-                multiply(j)
-            if j >= 2:
-                scale_pert(j - 1)
+            for j, m in passes_of_step(s):
+                multiply(j, (m,))
+            for j, m in passes_of_step(s - 1):
+                if m == 1:
+                    scale_pert(j)
             sort_words(2 * s + 2, False)
-            bias_term(s - 2)
+            for j, m in passes_of_step(s):
+                if m == 1:
+                    bias_term(2 * j)
+                    bias_term(2 * j + 1)
             spread_copy(s)
-            if j >= 1:
-                finish(j - 1)
+            for j, m in passes_of_step(s - 1):
+                if m == 0:
+                    finish(j)
             sort_words(2 * s + 3, False)
-        scale_pert(N_MRUNS - 1)
-        finish(N_MRUNS - 1)

from contextlib import ExitStack

import concourse.mybir as mybir
from concourse.masks import make_identity

B, IN, OUT = 512, 2048, 2048
FLOPS = 2 * 2 * B * IN * OUT
Y_SCALE = 170.0

F32 = mybir.dt.float32
BF16 = mybir.dt.bfloat16
U32 = mybir.dt.uint32
U8 = mybir.dt.uint8
FP8X4 = mybir.dt.float8_e4m3fn_x4
FP8 = mybir.dt.float8_e4m3fn
ALU = mybir.AluOpType
ACT = mybir.ActivationFunctionType

P = 128
PASSES = IN // 512
X_TILES = B // P
CHUNK = 256
N_CHUNKS = OUT // CHUNK
N_UNITS = 2 + 2 * N_CHUNKS
N_MRUNS = 2 * N_CHUNKS
N_STEPS = N_MRUNS + 4
D_COLS = 256
N_D = X_TILES * OUT // D_COLS

HEAD_PASSES = {2: [(0, 1)], 3: [(0, 0)], 4: [(1, 1)], 5: [(1, 0)]}
UNSORTED_UNITS = (0, 1,)
FIRST_SORTED_UNIT = 1
FIRST_SCALAR_SORT = 13

RAW_TILES = 12
SORTED_TILES = 6
GROUPED_TILES = 3
CODE_TILES = 4
T_TILES = 2
RESULT_TILES = 4
BYTE_TILES = 6


def tile_optimizedlinear_kernel(tc, input_data, weight, bias, prev_grad, prev_bias_grad, lr_samples, out_0, out_1):
    nc = tc.nc

    units = [("x", 0, input_data, 0), ("g", 0, prev_grad, 0), ("w", 0, weight, 0), ("x", 1, input_data, CHUNK)]
    for c in range(1, N_CHUNKS):
        units.append(("g", c, prev_grad, c * CHUNK))
        units.append(("w", c, weight, c * CHUNK))

    with ExitStack() as ctx:
        const = ctx.enter_context(tc.tile_pool(name="const", bufs=1))
        raw_pool = ctx.enter_context(tc.tile_pool(name="raw", bufs=RAW_TILES))
        sorted_pool = ctx.enter_context(tc.tile_pool(name="sorted", bufs=SORTED_TILES))
        grouped_pool = ctx.enter_context(tc.tile_pool(name="grouped", bufs=GROUPED_TILES))
        code_pool = ctx.enter_context(tc.tile_pool(name="codes", bufs=CODE_TILES))
        result_pool = ctx.enter_context(tc.tile_pool(name="result", bufs=T_TILES))
        turn_psum = ctx.enter_context(tc.psum_pool(name="turn", bufs=4))
        acc_psum = ctx.enter_context(tc.psum_pool(name="acc", bufs=4))
        ctx.enter_context(tc.manual_schedule())

        raw = {}
        by_parity = {}
        grouped = {}
        codes = {}
        acc = {}
        whole = {}
        t_tiles = {}
        spread_banks = {}
        progress = {"loaded": 0, "transposed": 0}

        def load_row_tile():
            n = progress["loaded"]
            if n >= 2 * N_UNITS or n - progress["transposed"] >= RAW_TILES:
                return
            progress["loaded"] += 1
            kind, index, src, first_row = units[n // 2]
            rows = slice(first_row + (n % 2) * P, first_row + (n % 2 + 1) * P)
            tile = raw_pool.tile([P, IN], BF16, name="raw")
            raw[n] = tile
            pieces = 2 if n == 0 else 1
            for q in range(pieces):
                cols = slice(q * IN // pieces, (q + 1) * IN // pieces)
                nc.sync.dma_start(out=tile[:, cols], in_=src[rows, cols])

        rows_in = const.tile([P, OUT], BF16, name="rows_in")
        lr_bf16 = const.tile([P, X_TILES], BF16, name="lr_bf16")
        nc.scalar.dma_start(out=rows_in[0:1, :], in_=prev_bias_grad.rearrange("(a b) -> a b", a=1))
        nc.scalar.dma_start(out=rows_in[32:33, :], in_=bias.rearrange("(a b) -> a b", a=1))
        with nc.allow_non_contiguous_dma(reason="lr_samples, one value to a partition: 512 elements in all"):
            nc.scalar.dma_start(out=lr_bf16[:], in_=lr_samples.rearrange("(i p) -> p i", p=P))
        for n in range(RAW_TILES):
            load_row_tile()

        selector = const.tile([P, 2, P], BF16, name="selector")
        vectors = const.tile([P, OUT], BF16, name="vectors")
        nc.vector.memset(selector[:], 0.0)
        nc.vector.memset(selector[0:32, 0, :], 1.0)
        nc.vector.memset(selector[32:64, 1, :], 1.0)
        nc.vector.memset(vectors[:], 0.0)
        identity = const.tile([P, P], F32, name="identity")
        make_identity(nc, identity[:])
        lr = const.tile([P, X_TILES], F32, name="lr")
        dummy_in = const.tile([P, 1], F32, name="dummy_in")
        nc.vector.memset(dummy_in[:], 0.0)
        dummy_out = const.tile([P, 1], F32, name="dummy_out")
        nc.scalar.activation(out=dummy_out[:], in_=dummy_in[:], func=ACT.Copy, scale=1.0)
        nc.vector.tensor_copy(out=vectors[0:1, :], in_=rows_in[0:1, :])
        nc.vector.tensor_copy(out=vectors[32:33, :], in_=rows_in[32:33, :])
        nc.vector.tensor_copy(out=lr[:], in_=lr_bf16[:])
        spread = const.tile([P, 2, OUT], BF16, name="spread")
        d_sbuf = const.tile([P, X_TILES, OUT], F32, name="d_sbuf")

        def sorted_by_scalar(n):
            return n >= FIRST_SCALAR_SORT and n % 2 == 1 and (n // 2) % 3 != 0

        def sort_words(n, on_scalar):
            if n >= 2 * N_UNITS or n // 2 in UNSORTED_UNITS or sorted_by_scalar(n) != on_scalar:
                return
            view = raw[n][:].bitcast(F32).rearrange("p (g j v) -> p g v j", g=PASSES, v=2)
            if on_scalar:
                tile = sorted_pool.tile([P, PASSES, 2, P], F32, name="by_parity_s", bufs=2)
                nc.scalar.copy(out=tile[:], in_=view)
            else:
                tile = sorted_pool.tile([P, PASSES, 2, P], F32, name="by_parity")
                nc.vector.tensor_copy(out=tile[:], in_=view)
            by_parity[n] = tile

        def transpose_unit(u):
            tile = grouped_pool.tile([P, PASSES * CHUNK * 4], BF16, name="grouped", align_bytes=64)
            grouped[u] = tile
            words = tile[:].bitcast(F32).rearrange("p (g r v) -> p g r v", g=PASSES, v=2)
            for t in range(2):
                for half in range(2):
                    bank = turn_psum.tile([P, 4, P], F32, name="bank")
                    for g2 in range(2):
                        g = 2 * half + g2
                        for v in range(2):
                            if 2 * u + t in by_parity:
                                src = by_parity[2 * u + t][:, g, v, :]
                            else:
                                src = raw[2 * u + t][:].bitcast(F32)[:, 256 * g + v:256 * (g + 1):2]
                            nc.tensor.transpose(bank[:, 2 * g2 + v, :], src, identity[:])
                    nc.scalar.copy(out=words[:, 2 * half:2 * half + 2, t * P:(t + 1) * P, :],
                                   in_=bank[:].rearrange("p (g v) r -> p g r v", v=2))
            progress["transposed"] = 2 * u + 2

        def quantize_unit(u):
            kind, index = units[u][0], units[u][1]
            bufs = 2 if kind == "x" else CODE_TILES
            cod = code_pool.tile([P, PASSES * CHUNK], U32, name=kind + "_codes", bufs=bufs, align_bytes=256)
            scl = code_pool.tile([P, PASSES * CHUNK], U8, name=kind + "_scales", bufs=bufs, align_bytes=256)
            codes[(kind, index)] = (cod, scl)
            nc.vector.quantize_mx(out=cod[:].bitcast(FP8X4), scales=scl[:], in_=grouped[u][:])

        def spread_matmuls(n):
            if n >= 4:
                return
            bank = turn_psum.tile([P, OUT // 2], BF16, name="bank")
            spread_banks[n] = bank
            for q in range(2):
                nc.tensor.matmul(out=bank[:, q * 512:(q + 1) * 512], lhsT=selector[:, n % 2, :],
                                 rhs=vectors[:, (n // 2) * 1024 + q * 512:(n // 2) * 1024 + (q + 1) * 512], start=True, stop=True)

        def spread_copy(n):
            if n >= 4:
                return
            nc.scalar.copy(out=spread[:, n % 2, (n // 2) * 1024:(n // 2 + 1) * 1024], in_=spread_banks[n][:])

        def bias_term(n):
            if n < 0 or n >= N_D:
                return
            i, cols = n % X_TILES, slice((n // X_TILES) * D_COLS, (n // X_TILES + 1) * D_COLS)
            nc.vector.scalar_tensor_tensor(out=d_sbuf[:, i, cols], in0=spread[:, 0, cols], scalar=lr[:, i:i + 1],
                                           in1=spread[:, 1, cols], op0=ALU.mult, op1=ALU.subtract)

        def multiply(j, halves=(1, 0)):
            c, h = j // 2, j % 2
            x_cod, x_scl = codes[("x", h)]
            last = j == N_MRUNS - 1
            for m in halves:
                if last and m == 0:
                    first = turn_psum.tile([P, CHUNK], F32, name="bank")
                    second = turn_psum.tile([P, CHUNK], F32, name="bank")
                    acc[(j, m, 0)], acc[(j, m, 1)] = first[:], second[:]
                else:
                    bank = acc_psum.tile([P, 2, CHUNK], F32, name="acc")
                    acc[(j, m, 0)], acc[(j, m, 1)] = bank[:, 0, :], bank[:, 1, :]
                    whole[(j, m)] = bank[:]
                w_cod, w_scl = codes[("wg"[m], c)]
                for t in range(2):
                    for g in range(PASSES):
                        x_cols = slice(g * CHUNK + t * P, g * CHUNK + (t + 1) * P)
                        w_cols = slice(g * CHUNK, (g + 1) * CHUNK)
                        nc.tensor.matmul_mx(out=acc[(j, m, t)], lhsT=x_cod[:, x_cols].bitcast(FP8X4), lhsT_scale=x_scl[:, x_cols],
                                            rhs=w_cod[:, w_cols].bitcast(FP8X4), rhs_scale=w_scl[:, w_cols],
                                            start=(g == 0), stop=(g == PASSES - 1))

        def scale_pert(j):
            c, h = j // 2, j % 2
            tile = result_pool.tile([P, 2, CHUNK], F32, name="t")
            t_tiles[j] = tile
            for t in range(2):
                i = 2 * h + t
                nc.vector.scalar_tensor_tensor(out=tile[:, t, :], in0=acc[(j, 1, t)], scalar=lr[:, i:i + 1],
                                               in1=d_sbuf[:, i, c * CHUNK:(c + 1) * CHUNK], op0=ALU.mult, op1=ALU.add)

        def finish(j):
            c, h = j // 2, j % 2
            cols = slice(c * CHUNK, (c + 1) * CHUNK)
            result = result_pool.tile([P, 2, CHUNK], F32, name="result", bufs=RESULT_TILES)
            as_fp8 = result_pool.tile([P, 2, CHUNK], FP8, name="as_fp8", bufs=BYTE_TILES)
            if (j, 0) in whole:
                rows = slice(2 * h * P, (2 * h + 2) * P)
                nc.vector.tensor_tensor(out=result[:], in0=whole[(j, 0)], in1=t_tiles[j][:], op=ALU.subtract)
                nc.scalar.activation(out=as_fp8[:], in_=result[:], func=ACT.Copy, scale=Y_SCALE, saturate=False)
                nc.sync.dma_start(out=out_0[rows, cols].rearrange("(t p) c -> p t c", p=P), in_=result[:])
                nc.sync.dma_start(out=out_1[rows, cols].rearrange("(t p) c -> p t c", p=P), in_=as_fp8[:].bitcast(U8))
            else:
                for t in range(2):
                    rows = slice((2 * h + t) * P, (2 * h + t + 1) * P)
                    nc.vector.tensor_tensor(out=result[:, t, :], in0=acc[(j, 0, t)], in1=t_tiles[j][:, t, :], op=ALU.subtract)
                    nc.scalar.activation(out=as_fp8[:, t, :], in_=result[:, t, :], func=ACT.Copy, scale=Y_SCALE, saturate=False)
                    nc.sync.dma_start(out=out_0[rows, cols], in_=result[:, t, :])
                    nc.sync.dma_start(out=out_1[rows, cols], in_=as_fp8[:, t, :].bitcast(U8))

        def passes_of_step(s):
            if s in HEAD_PASSES:
                return HEAD_PASSES[s]
            j = s - 4 if s >= 5 else -1
            return [(j, 1), (j, 0)] if 0 <= j < N_MRUNS else []

        for s in range(N_STEPS + 1):
            if s < N_UNITS:
                transpose_unit(s)
                spread_matmuls(s)
                load_row_tile()
                load_row_tile()
            for n in (2 * s + 4, 2 * s + 5):
                sort_words(n, True)
            if 1 <= s <= N_UNITS:
                quantize_unit(s - 1)
            for j, m in passes_of_step(s):
                multiply(j, (m,))
            for j, m in passes_of_step(s - 1):
                if m == 1:
                    scale_pert(j)
            sort_words(2 * s + 2, False)
            for j, m in passes_of_step(s):
                if m == 1:
                    bias_term(2 * j)
                    bias_term(2 * j + 1)
            spread_copy(s)
            for j, m in passes_of_step(s - 1):
                if m == 0:
                    finish(j)
            sort_words(2 * s + 3, False)
